import numpy as np
import ml_dtypes


def mxq(x, axis, fmt="e4m3"):
    dtype, down = {"e4m3": (ml_dtypes.float8_e4m3fn, 7), "e5m2": (ml_dtypes.float8_e5m2, 14)}[fmt]
    v = np.moveaxis(np.asarray(x, np.float32).astype(ml_dtypes.bfloat16).astype(np.float64), axis, -1)
    blocks = v.reshape(v.shape[:-1] + (-1, 32))
    amax = np.abs(blocks).max(-1, keepdims=True)
    byte = np.maximum(np.where(amax > 0, np.frexp(amax)[1] - 1 + 127, 0) - down, 1)
    scale = np.exp2(byte - 127.0)
    codes = (blocks / scale).astype(np.float32).astype(dtype).astype(np.float64)
    return np.moveaxis((codes * scale).reshape(v.shape), -1, axis)


WIDE = False


def mx_kscale(k):
    if not WIDE:
        return np.ones(k)
    levels = np.array([10, -10, 5, -5, 0])
    a = np.random.permutation(np.resize(levels, k // 512 * 4)).reshape(k // 512, 4)
    idx = np.arange(k)
    return np.exp2(a[idx // 512, idx % 128 // 32])


BF16 = ml_dtypes.bfloat16


def bf(x):
    return np.asarray(x, np.float32).astype(BF16)


def f64(x):
    return np.asarray(x).astype(np.float64)


E2M1 = np.array([0.0, 0.5, 1.0, 1.5, 2.0, 3.0, 4.0, 6.0, -0.0, -0.5, -1.0, -1.5, -2.0, -3.0, -4.0, -6.0])


def pack_weight(w, fmt):
    k, n = w.shape
    w = f64(bf(w)).reshape(k // 32, 32, n)
    amax = np.abs(w).max(1)
    if fmt == "e4m3":
        byte = np.frexp(amax)[1] - 1 + 127 - 7
    else:
        mant, ex = np.frexp(amax / 6.0)
        byte = np.where(mant > 0.5, ex, ex - 1) + 127
    byte = np.clip(np.where(amax > 0, byte, 1), 1, 254)
    scaled = (w * np.exp2(127.0 - byte)[:, None, :]).reshape(k, n).astype(np.float32)
    by_word = np.ascontiguousarray(scaled.reshape(k // 512, 128, 4, n).transpose(0, 1, 3, 2))
    if fmt == "e4m3":
        words = by_word.astype(ml_dtypes.float8_e4m3fn).view(np.uint8)
    else:
        c = by_word.astype(ml_dtypes.float4_e2m1fn).view(np.uint8) & 0xF
        words = c[..., 0::2] | (c[..., 1::2] << 4)
    return np.ascontiguousarray(words), np.ascontiguousarray(byte.astype(np.uint8).reshape(k // 512, 16, n))


def unpack_weight(words, scales, fmt):
    g, p, n, _ = words.shape
    if fmt == "e4m3":
        vals = np.ascontiguousarray(words).view(ml_dtypes.float8_e4m3fn).astype(np.float64)
    else:
        nib = np.empty((g, p, n, 4), np.uint8)
        nib[..., 0::2] = words & 0xF
        nib[..., 1::2] = words >> 4
        vals = E2M1[nib]
    vals = vals * np.repeat(np.exp2(scales.astype(np.float64) - 127.0), 8, axis=1)[..., None]
    return vals.transpose(0, 1, 3, 2).reshape(g * 512, n)


B, S, D, H, KD, VD = 32, 32, 1024, 8, 128, 128
E = H * VD
EPS = 1e-5
FMT = "e4m3"


def silu(v):
    return v / (1.0 + np.exp(-v))


def setup_inputs():
    s = mx_kscale(D)
    amp = 10.0 ** np.random.uniform(-2.5, 0.5, (B, S, H, 1))
    ret = amp * (np.random.standard_normal((B, S, H, VD)) + 0.3 * np.random.standard_normal((B, S, H, 1)))
    x = bf(np.random.standard_normal((B, S, D)) * s)
    ret_cat = bf(ret.reshape(B, S, E))
    Wg_words, Wg_scales = pack_weight(np.random.standard_normal((D, E)) / np.sqrt(D) / s[:, None], FMT)
    bg = bf(np.random.standard_normal(E) * 0.2)
    Wo_words, Wo_scales = pack_weight(np.random.standard_normal((E, D)) / np.sqrt(E), FMT)
    bo = bf(np.random.standard_normal(D) * 0.2)
    return {"x": x,
            "ret_cat": ret_cat,
            "Wg_words": Wg_words,
            "Wg_scales": Wg_scales,
            "bg": bg,
            "Wo_words": Wo_words,
            "Wo_scales": Wo_scales,
            "bo": bo}


def reference(x, ret_cat, Wg_words, Wg_scales, bg, Wo_words, Wo_scales, bo):
    gate = silu((mxq(f64(x), 2, "e4m3") @ unpack_weight(Wg_words, Wg_scales, FMT)) + f64(bg))
    g = f64(ret_cat).reshape(B * S, H, VD)
    mu = g.mean(-1, keepdims=True)
    var = g.var(-1, keepdims=True)
    cat = ((g - mu) / np.sqrt(var + EPS)).reshape(B, S, E)
    h = gate * cat
    return (mxq(h, 2, "e4m3") @ unpack_weight(Wo_words, Wo_scales, FMT)) + f64(bo)

@@ -1,0 +1,256 @@
+from contextlib import ExitStack
+
+import concourse.mybir as mybir
+from concourse.masks import make_identity
+
+F32 = mybir.dt.float32
+BF16 = mybir.dt.bfloat16
+I32 = mybir.dt.int32
+U32 = mybir.dt.uint32
+U8 = mybir.dt.uint8
+FP8X4 = mybir.dt.float8_e4m3fn_x4
+ALU = mybir.AluOpType
+ACT = mybir.ActivationFunctionType
+
+P = 128
+PACK = 4
+K_PASS = P * PACK
+BANK = 512
+TOKENS = 32 * 32
+WIDTH = 1024
+HEADS = 8
+HEAD = WIDTH // HEADS
+TILES = TOKENS // P
+GROUPS = WIDTH // K_PASS
+HEADS_PER_GROUP = HEADS // GROUPS
+QUARTER = HEAD // PACK
+EPS = 1e-5
+
+FLOPS = 2 * 2 * TOKENS * WIDTH * WIDTH
+
+
+def tile_gatedmultiscaleretentionlayer_pa_kernel(
+    tc, x, ret_cat, Wg_words, Wg_scales, bg, Wo_words, Wo_scales, bo, out
+):
+    nc = tc.nc
+
+    x_rows = x.flatten_outer_dims().rearrange("(p i) d -> p i d", i=TILES)
+    ret_rows = ret_cat.flatten_outer_dims().rearrange("(p i) d -> p i d", i=TILES)
+    out_rows = out.flatten_outer_dims().rearrange("(p i) d -> p i d", i=TILES)
+
+    with ExitStack() as stack:
+        const = stack.enter_context(tc.tile_pool(name="const", bufs=1))
+        small = stack.enter_context(tc.tile_pool(name="small", bufs=3))
+        work = stack.enter_context(tc.tile_pool(name="work", bufs=2))
+        ahead = stack.enter_context(tc.tile_pool(name="ahead", bufs=4))
+        psum_t = stack.enter_context(tc.psum_pool(name="psum_t", bufs=1))
+        psum_mm = stack.enter_context(tc.psum_pool(name="psum_mm", bufs=3))
+
+        planes = const.tile([P, WIDTH], U8, align_bytes=64)
+        nc.vector.memset(planes[:].bitcast(I32), 0)
+
+        x_sb = [const.tile([P, WIDTH], BF16, name="x%d" % i) for i in range(TILES)]
+        ret_sb = [const.tile([P, WIDTH], BF16, name="ret%d" % i) for i in range(TILES)]
+        wg_words = const.tile([P, GROUPS, WIDTH], U32, align_bytes=64)
+        wo_words = const.tile([P, GROUPS, WIDTH], U32, align_bytes=64)
+
+        def load_tokens(i):
+            nc.sync.dma_start(out=ret_sb[i][:], in_=ret_rows[:, i, :])
+            nc.sync.dma_start(out=x_sb[i][:], in_=x_rows[:, i, :])
+
+        def load_weight(words_sb, words, scales, first_plane):
+            for quadrant in range(4):
+                top = 32 * quadrant + PACK * first_plane
+                nc.sync.dma_start(
+                    out=planes[top : top + PACK * GROUPS, :].bitcast(I32),
+                    in_=scales[:, 4 * quadrant : 4 * quadrant + 4, :].bitcast(I32),
+                )
+            for g in range(GROUPS):
+                nc.sync.dma_start(
+                    out=words_sb[:, g, :].bitcast(I32),
+                    in_=words[g].rearrange("p n t -> p (n t)").bitcast(I32),
+                )
+
+        load_tokens(0)
+        load_weight(wg_words, Wg_words, Wg_scales, 0)
+        load_tokens(1)
+        load_weight(wo_words, Wo_words, Wo_scales, GROUPS)
+        for i in range(2, TILES):
+            load_tokens(i)
+
+        bias_rows = const.tile([P, 2 * WIDTH], BF16)
+        nc.vector.memset(bias_rows[:].bitcast(I32), 0)
+        nc.gpsimd.dma_start(out=bias_rows[0:1, 0:WIDTH], in_=bg.unsqueeze(0))
+        nc.gpsimd.dma_start(out=bias_rows[0:1, WIDTH : 2 * WIDTH], in_=bo.unsqueeze(0))
+        ones = const.tile([P, P], BF16)
+        nc.vector.memset(ones[:], 1.0)
+        minus_half = const.tile([P, HEADS], F32)
+        nc.vector.memset(minus_half[:], -0.5)
+
+        warm = const.tile([P, 1], F32)
+        nc.scalar.activation(out=warm[:], in_=minus_half[:, 0:1], func=ACT.Silu)
+
+        ident_f32 = const.tile([P, P], F32)
+        make_identity(nc, ident_f32[:])
+        ident_bf16 = const.tile([P, P], BF16)
+        make_identity(nc, ident_bf16[:])
+
+        bg_sorted = const.tile([P, GROUPS, PACK, P], F32)
+        bo_all = const.tile([P, GROUPS, BANK], F32)
+        for g in range(GROUPS):
+            spread = psum_mm.tile([P, BANK], F32, tag="z")
+            nc.tensor.matmul(
+                out=spread[:], lhsT=ones[:], rhs=bias_rows[:, g * BANK : (g + 1) * BANK],
+                start=True, stop=True,
+            )
+            nc.vector.tensor_copy(
+                out=bg_sorted[:, g], in_=spread[:].rearrange("p (c t) -> p t c", t=PACK)
+            )
+        for g in range(GROUPS):
+            spread = psum_mm.tile([P, BANK], F32, tag="o")
+            nc.tensor.matmul(
+                out=spread[:], lhsT=ones[:],
+                rhs=bias_rows[:, WIDTH + g * BANK : WIDTH + (g + 1) * BANK],
+                start=True, stop=True,
+            )
+            nc.vector.tensor_copy(out=bo_all[:, g], in_=spread[:])
+
+        cat_of = {}
+        xq_of = {}
+        h_of = {}
+        hq_of = {}
+
+        def norm(i):
+            stats = small.tile([P, HEADS, 6], F32)
+            for head in range(HEADS):
+                nc.vector.bn_stats(
+                    out=stats[:, head, :], in_=ret_sb[i][:, head * HEAD : (head + 1) * HEAD]
+                )
+            mean_even, m2_even = stats[:, :, 1], stats[:, :, 2]
+            mean_odd, m2_odd = stats[:, :, 4], stats[:, :, 5]
+            gap = small.tile([P, HEADS], F32)
+            nc.vector.tensor_tensor(out=gap[:], in0=mean_even, in1=mean_odd, op=ALU.subtract)
+            gap_sq = small.tile([P, HEADS], F32)
+            nc.vector.scalar_tensor_tensor(
+                out=gap_sq[:], in0=gap[:], scalar=0.25, in1=gap[:], op0=ALU.mult, op1=ALU.mult
+            )
+            m2 = small.tile([P, HEADS], F32)
+            nc.vector.scalar_tensor_tensor(
+                out=m2[:], in0=m2_even, scalar=HEAD * EPS, in1=m2_odd, op0=ALU.add, op1=ALU.add
+            )
+            var_eps = small.tile([P, HEADS], F32)
+            nc.vector.scalar_tensor_tensor(
+                out=var_eps[:], in0=m2[:], scalar=1.0 / HEAD, in1=gap_sq[:],
+                op0=ALU.mult, op1=ALU.add,
+            )
+            mean2 = small.tile([P, HEADS], F32)
+            nc.vector.tensor_tensor(out=mean2[:], in0=mean_even, in1=mean_odd, op=ALU.add)
+            rstd = small.tile([P, HEADS], F32)
+            nc.gpsimd.tensor_tensor(out=rstd[:], in0=var_eps[:], in1=minus_half[:], op=ALU.pow)
+            shift = small.tile([P, HEADS], F32)
+            nc.vector.scalar_tensor_tensor(
+                out=shift[:], in0=mean2[:], scalar=-0.5, in1=rstd[:], op0=ALU.mult, op1=ALU.mult
+            )
+            cat = ahead.tile([P, GROUPS, PACK, P], F32)
+            for head in range(HEADS):
+                g, j = divmod(head, HEADS_PER_GROUP)
+                nc.scalar.activation(
+                    out=cat[:, g, :, j * QUARTER : (j + 1) * QUARTER],
+                    in_=ret_sb[i][:, head * HEAD : (head + 1) * HEAD].rearrange(
+                        "p (c t) -> p t c", t=PACK
+                    ),
+                    func=ACT.Identity,
+                    scale=rstd[:, head : head + 1],
+                    bias=shift[:, head : head + 1],
+                )
+            cat_of[i] = cat
+
+        def quantise(grouped, label):
+            words = work.tile([P, GROUPS * P], U32, align_bytes=64, name=label + "_words")
+            scales = work.tile([P, GROUPS * P], U8, align_bytes=64, name=label + "_scales")
+            nc.vector.quantize_mx(out=words[:].bitcast(FP8X4), scales=scales[:], in_=grouped[:])
+            return words, scales
+
+        def transpose_x(i):
+            x_words = x_sb[i][:].bitcast(F32)
+            pairs = K_PASS // 2
+            xt = psum_t.tile([P, GROUPS, 2, P], F32)
+            for g in range(GROUPS):
+                for u in range(2):
+                    nc.tensor.transpose(
+                        out=xt[:, g, u, :],
+                        in_=x_words[:, g * pairs + u : (g + 1) * pairs : 2],
+                        identity=ident_f32[:],
+                    )
+            x_grouped = work.tile([P, GROUPS * P * PACK], BF16, align_bytes=64)
+            nc.scalar.copy(
+                out=x_grouped[:].bitcast(F32).rearrange("p (g r u) -> p g r u", g=GROUPS, u=2),
+                in_=xt[:].rearrange("p g u r -> p g r u"),
+            )
+            xq_of[i] = quantise(x_grouped, "xq")
+
+        def mx_product(banks, lhs, weight_words, first_plane):
+            words, scales = lhs
+            for n in range(GROUPS):
+                for g in range(GROUPS):
+                    nc.tensor.matmul_mx(
+                        out=banks[n][:],
+                        lhsT=words[:, g * P : (g + 1) * P].bitcast(FP8X4),
+                        lhsT_scale=scales[:, g * P : (g + 1) * P],
+                        rhs=weight_words[:, g, n * BANK : (n + 1) * BANK].bitcast(FP8X4),
+                        rhs_scale=planes[PACK * (first_plane + g) : P, n * BANK : (n + 1) * BANK],
+                        start=(g == 0),
+                        stop=(g == GROUPS - 1),
+                    )
+
+        def gate_times_cat(i):
+            z = [psum_mm.tile([P, BANK], F32, name="z%d" % n, tag="z") for n in range(GROUPS)]
+            mx_product(z, xq_of[i], wg_words, 0)
+            cat = cat_of[i]
+            biased = work.tile([P, GROUPS, PACK, P], F32)
+            gate = work.tile([P, GROUPS, PACK, P], F32)
+            h = work.tile([P, GROUPS, PACK, P], BF16)
+            for n in range(GROUPS):
+                nc.vector.tensor_tensor(
+                    out=biased[:, n], in0=z[n][:].rearrange("p (c t) -> p t c", t=PACK),
+                    in1=bg_sorted[:, n], op=ALU.add,
+                )
+                nc.scalar.activation(out=gate[:, n], in_=biased[:, n], func=ACT.Silu)
+                nc.gpsimd.tensor_tensor(out=h[:, n], in0=gate[:, n], in1=cat[:, n], op=ALU.mult)
+            h_of[i] = h
+
+        def transpose_h(i):
+            h = h_of[i]
+            ht = psum_t.tile([P, GROUPS, PACK, P], BF16)
+            for g in range(GROUPS):
+                for t in range(PACK):
+                    nc.tensor.transpose(out=ht[:, g, t, :], in_=h[:, g, t, :], identity=ident_bf16[:])
+            h_grouped = work.tile([P, GROUPS * P * PACK], BF16, align_bytes=64)
+            nc.scalar.copy(
+                out=h_grouped[:].rearrange("p (g r t) -> p g r t", g=GROUPS, t=PACK),
+                in_=ht[:].rearrange("p g t r -> p g r t"),
+            )
+            hq_of[i] = quantise(h_grouped, "hq")
+
+        def project(i):
+            o = [psum_mm.tile([P, BANK], F32, name="o%d" % n, tag="o") for n in range(GROUPS)]
+            mx_product(o, hq_of[i], wo_words, GROUPS)
+            for n in range(GROUPS):
+                result = ahead.tile([P, BANK], F32)
+                nc.vector.tensor_tensor(out=result[:], in0=o[n][:], in1=bo_all[:, n], op=ALU.add)
+                nc.sync.dma_start(out=out_rows[:, i, n * BANK : (n + 1) * BANK], in_=result[:])
+
+        norm(0)
+        transpose_x(0)
+        norm(1)
+        for r in range(TILES + 1):
+            if r >= 1:
+                transpose_h(r - 1)
+            if r + 1 < TILES:
+                transpose_x(r + 1)
+            if r < TILES:
+                gate_times_cat(r)
+            if r >= 1:
+                project(r - 1)
+            if r + 2 < TILES:
+                norm(r + 2)

@@ -42,9 +42,12 @@ def tile_gatedmultiscaleretentionlayer_pa_kernel(
         const = stack.enter_context(tc.tile_pool(name="const", bufs=1))
         small = stack.enter_context(tc.tile_pool(name="small", bufs=3))
         work = stack.enter_context(tc.tile_pool(name="work", bufs=2))
-        ahead = stack.enter_context(tc.tile_pool(name="ahead", bufs=4))
-        psum_t = stack.enter_context(tc.psum_pool(name="psum_t", bufs=1))
-        psum_mm = stack.enter_context(tc.psum_pool(name="psum_mm", bufs=3))
+        halves = stack.enter_context(tc.tile_pool(name="halves", bufs=4))
+        psum_xt = stack.enter_context(tc.psum_pool(name="psum_xt", bufs=1))
+        psum_ht = stack.enter_context(tc.psum_pool(name="psum_ht", bufs=2))
+        psum_z = stack.enter_context(tc.psum_pool(name="psum_z", bufs=3))
+        psum_o = stack.enter_context(tc.psum_pool(name="psum_o", bufs=2))
+        stack.enter_context(tc.manual_schedule())
 
         planes = const.tile([P, WIDTH], U8, align_bytes=64)
         nc.vector.memset(planes[:].bitcast(I32), 0)
@@ -54,29 +57,47 @@ def tile_gatedmultiscaleretentionlayer_pa_kernel(
         wg_words = const.tile([P, GROUPS, WIDTH], U32, align_bytes=64)
         wo_words = const.tile([P, GROUPS, WIDTH], U32, align_bytes=64)
 
-        def load_tokens(i):
-            nc.sync.dma_start(out=ret_sb[i][:], in_=ret_rows[:, i, :])
+        def load_x(i):
             nc.sync.dma_start(out=x_sb[i][:], in_=x_rows[:, i, :])
 
-        def load_weight(words_sb, words, scales, first_plane):
+        def load_ret(i):
+            nc.sync.dma_start(out=ret_sb[i][:], in_=ret_rows[:, i, :])
+
+        def load_scales(scales, first_plane):
             for quadrant in range(4):
                 top = 32 * quadrant + PACK * first_plane
                 nc.sync.dma_start(
                     out=planes[top : top + PACK * GROUPS, :].bitcast(I32),
                     in_=scales[:, 4 * quadrant : 4 * quadrant + 4, :].bitcast(I32),
                 )
+
+        def load_words(words_sb, words, n):
             for g in range(GROUPS):
                 nc.sync.dma_start(
-                    out=words_sb[:, g, :].bitcast(I32),
-                    in_=words[g].rearrange("p n t -> p (n t)").bitcast(I32),
+                    out=words_sb[:, g, n * BANK : (n + 1) * BANK].bitcast(I32),
+                    in_=words[g, :, n * BANK : (n + 1) * BANK, :]
+                    .rearrange("p n t -> p (n t)")
+                    .bitcast(I32),
                 )
 
-        load_tokens(0)
-        load_weight(wg_words, Wg_words, Wg_scales, 0)
-        load_tokens(1)
-        load_weight(wo_words, Wo_words, Wo_scales, GROUPS)
-        for i in range(2, TILES):
-            load_tokens(i)
+        load_ret(0)
+        load_x(0)
+        load_ret(1)
+        load_scales(Wg_scales, 0)
+        load_words(wg_words, Wg_words, 0)
+        load_x(1)
+        load_words(wg_words, Wg_words, 1)
+        load_ret(2)
+        load_x(2)
+        load_scales(Wo_scales, GROUPS)
+        load_words(wo_words, Wo_words, 0)
+        load_words(wo_words, Wo_words, 1)
+        for i in range(3, TILES):
+            load_ret(i)
+            load_x(i)
+
+        ident_f32 = const.tile([P, P], F32)
+        make_identity(nc, ident_f32[:])
 
         bias_rows = const.tile([P, 2 * WIDTH], BF16)
         nc.vector.memset(bias_rows[:].bitcast(I32), 0)
@@ -87,40 +108,38 @@ def tile_gatedmultiscaleretentionlayer_pa_kernel(
         minus_half = const.tile([P, HEADS], F32)
         nc.vector.memset(minus_half[:], -0.5)
 
-        warm = const.tile([P, 1], F32)
-        nc.scalar.activation(out=warm[:], in_=minus_half[:, 0:1], func=ACT.Silu)
-
-        ident_f32 = const.tile([P, P], F32)
-        make_identity(nc, ident_f32[:])
         ident_bf16 = const.tile([P, P], BF16)
         make_identity(nc, ident_bf16[:])
 
+        warm = const.tile([P, 1], F32)
+        nc.scalar.activation(out=warm[:], in_=minus_half[:, 0:1], func=ACT.Silu)
+
         bg_sorted = const.tile([P, GROUPS, PACK, P], F32)
         bo_all = const.tile([P, GROUPS, BANK], F32)
-        for g in range(GROUPS):
-            spread = psum_mm.tile([P, BANK], F32, tag="z")
-            nc.tensor.matmul(
-                out=spread[:], lhsT=ones[:], rhs=bias_rows[:, g * BANK : (g + 1) * BANK],
-                start=True, stop=True,
-            )
-            nc.vector.tensor_copy(
-                out=bg_sorted[:, g], in_=spread[:].rearrange("p (c t) -> p t c", t=PACK)
-            )
-        for g in range(GROUPS):
-            spread = psum_mm.tile([P, BANK], F32, tag="o")
-            nc.tensor.matmul(
-                out=spread[:], lhsT=ones[:],
-                rhs=bias_rows[:, WIDTH + g * BANK : WIDTH + (g + 1) * BANK],
-                start=True, stop=True,
-            )
-            nc.vector.tensor_copy(out=bo_all[:, g], in_=spread[:])
 
-        cat_of = {}
-        xq_of = {}
-        h_of = {}
-        hq_of = {}
+        def spread_biases():
+            for g in range(GROUPS):
+                spread_bg = psum_z.tile([P, BANK], F32, tag="z")
+                nc.tensor.matmul(
+                    out=spread_bg[:], lhsT=ones[:], rhs=bias_rows[:, g * BANK : (g + 1) * BANK],
+                    start=True, stop=True,
+                )
+                nc.scalar.copy(
+                    out=bg_sorted[:, g], in_=spread_bg[:].rearrange("p (c t) -> p t c", t=PACK)
+                )
+            for g in range(GROUPS):
+                spread_bo = psum_o.tile([P, BANK], F32, tag="o")
+                nc.tensor.matmul(
+                    out=spread_bo[:], lhsT=ones[:],
+                    rhs=bias_rows[:, WIDTH + g * BANK : WIDTH + (g + 1) * BANK],
+                    start=True, stop=True,
+                )
+                nc.vector.tensor_copy(out=bo_all[:, g], in_=spread_bo[:])
 
-        def norm(i):
+        moments_of, affine_of, cat_of = {}, {}, {}
+        xq_of, z_of, biased_of, gate_of, h_of, hq_of, o_of = {}, {}, {}, {}, {}, {}, {}
+
+        def statistics(i):
             stats = small.tile([P, HEADS, 6], F32)
             for head in range(HEADS):
                 nc.vector.bn_stats(
@@ -143,15 +162,24 @@ def tile_gatedmultiscaleretentionlayer_pa_kernel(
                 out=var_eps[:], in0=m2[:], scalar=1.0 / HEAD, in1=gap_sq[:],
                 op0=ALU.mult, op1=ALU.add,
             )
-            mean2 = small.tile([P, HEADS], F32)
-            nc.vector.tensor_tensor(out=mean2[:], in0=mean_even, in1=mean_odd, op=ALU.add)
+            minus_mean = small.tile([P, HEADS], F32)
+            nc.vector.scalar_tensor_tensor(
+                out=minus_mean[:], in0=gap[:], scalar=-0.5, in1=mean_odd,
+                op0=ALU.mult, op1=ALU.subtract,
+            )
+            moments_of[i] = (var_eps, minus_mean)
+
+        def scale_and_shift(i):
+            var_eps, minus_mean = moments_of[i]
             rstd = small.tile([P, HEADS], F32)
             nc.gpsimd.tensor_tensor(out=rstd[:], in0=var_eps[:], in1=minus_half[:], op=ALU.pow)
             shift = small.tile([P, HEADS], F32)
-            nc.vector.scalar_tensor_tensor(
-                out=shift[:], in0=mean2[:], scalar=-0.5, in1=rstd[:], op0=ALU.mult, op1=ALU.mult
-            )
-            cat = ahead.tile([P, GROUPS, PACK, P], F32)
+            nc.gpsimd.tensor_tensor(out=shift[:], in0=minus_mean[:], in1=rstd[:], op=ALU.mult)
+            affine_of[i] = (rstd, shift)
+
+        def normalise(i):
+            rstd, shift = affine_of[i]
+            cat = work.tile([P, GROUPS, PACK, P], F32)
             for head in range(HEADS):
                 g, j = divmod(head, HEADS_PER_GROUP)
                 nc.scalar.activation(
@@ -165,16 +193,10 @@ def tile_gatedmultiscaleretentionlayer_pa_kernel(
                 )
             cat_of[i] = cat
 
-        def quantise(grouped, label):
-            words = work.tile([P, GROUPS * P], U32, align_bytes=64, name=label + "_words")
-            scales = work.tile([P, GROUPS * P], U8, align_bytes=64, name=label + "_scales")
-            nc.vector.quantize_mx(out=words[:].bitcast(FP8X4), scales=scales[:], in_=grouped[:])
-            return words, scales
-
         def transpose_x(i):
             x_words = x_sb[i][:].bitcast(F32)
             pairs = K_PASS // 2
-            xt = psum_t.tile([P, GROUPS, 2, P], F32)
+            xt = psum_xt.tile([P, GROUPS, 2, P], F32)
             for g in range(GROUPS):
                 for u in range(2):
                     nc.tensor.transpose(
@@ -187,70 +209,103 @@ def tile_gatedmultiscaleretentionlayer_pa_kernel(
                 out=x_grouped[:].bitcast(F32).rearrange("p (g r u) -> p g r u", g=GROUPS, u=2),
                 in_=xt[:].rearrange("p g u r -> p g r u"),
             )
-            xq_of[i] = quantise(x_grouped, "xq")
+            xq_words = work.tile([P, GROUPS, P], U32, align_bytes=64)
+            xq_scales = work.tile([P, GROUPS, P], U8, align_bytes=64)
+            nc.vector.quantize_mx(
+                out=xq_words[:].rearrange("p g r -> p (g r)").bitcast(FP8X4),
+                scales=xq_scales[:].rearrange("p g r -> p (g r)"),
+                in_=x_grouped[:],
+            )
+            xq_of[i] = [(xq_words[:, g, :], xq_scales[:, g, :]) for g in range(GROUPS)]
 
-        def mx_product(banks, lhs, weight_words, first_plane):
-            words, scales = lhs
-            for n in range(GROUPS):
-                for g in range(GROUPS):
-                    nc.tensor.matmul_mx(
-                        out=banks[n][:],
-                        lhsT=words[:, g * P : (g + 1) * P].bitcast(FP8X4),
-                        lhsT_scale=scales[:, g * P : (g + 1) * P],
-                        rhs=weight_words[:, g, n * BANK : (n + 1) * BANK].bitcast(FP8X4),
-                        rhs_scale=planes[PACK * (first_plane + g) : P, n * BANK : (n + 1) * BANK],
-                        start=(g == 0),
-                        stop=(g == GROUPS - 1),
-                    )
+        def mx_pass(bank, lhs, weight_words, first_plane, g, n):
+            words, scales = lhs[g]
+            nc.tensor.matmul_mx(
+                out=bank[:],
+                lhsT=words.bitcast(FP8X4),
+                lhsT_scale=scales,
+                rhs=weight_words[:, g, n * BANK : (n + 1) * BANK].bitcast(FP8X4),
+                rhs_scale=planes[PACK * (first_plane + g) : P, n * BANK : (n + 1) * BANK],
+                start=(g == 0),
+                stop=(g == GROUPS - 1),
+            )
 
-        def gate_times_cat(i):
-            z = [psum_mm.tile([P, BANK], F32, name="z%d" % n, tag="z") for n in range(GROUPS)]
-            mx_product(z, xq_of[i], wg_words, 0)
-            cat = cat_of[i]
+        def gate_matmul(i):
             biased = work.tile([P, GROUPS, PACK, P], F32)
-            gate = work.tile([P, GROUPS, PACK, P], F32)
-            h = work.tile([P, GROUPS, PACK, P], BF16)
             for n in range(GROUPS):
+                z = psum_z.tile([P, BANK], F32, tag="z")
+                for g in range(GROUPS):
+                    mx_pass(z, xq_of[i], wg_words, 0, g, n)
                 nc.vector.tensor_tensor(
-                    out=biased[:, n], in0=z[n][:].rearrange("p (c t) -> p t c", t=PACK),
+                    out=biased[:, n], in0=z[:].rearrange("p (c t) -> p t c", t=PACK),
                     in1=bg_sorted[:, n], op=ALU.add,
                 )
-                nc.scalar.activation(out=gate[:, n], in_=biased[:, n], func=ACT.Silu)
-                nc.gpsimd.tensor_tensor(out=h[:, n], in0=gate[:, n], in1=cat[:, n], op=ALU.mult)
+            biased_of[i] = biased
+
+        def silu(i):
+            gate = work.tile([P, GROUPS, PACK, P], F32)
+            for n in range(GROUPS):
+                nc.scalar.activation(out=gate[:, n], in_=biased_of[i][:, n], func=ACT.Silu)
+            gate_of[i] = gate
+
+        def product(i):
+            h = work.tile([P, GROUPS, PACK, P], BF16)
+            for n in range(GROUPS):
+                nc.gpsimd.tensor_tensor(
+                    out=h[:, n], in0=gate_of[i][:, n], in1=cat_of[i][:, n], op=ALU.mult
+                )
             h_of[i] = h
 
         def transpose_h(i):
-            h = h_of[i]
-            ht = psum_t.tile([P, GROUPS, PACK, P], BF16)
+            hq_of[i] = []
             for g in range(GROUPS):
+                ht = psum_ht.tile([P, PACK, P], BF16)
                 for t in range(PACK):
-                    nc.tensor.transpose(out=ht[:, g, t, :], in_=h[:, g, t, :], identity=ident_bf16[:])
-            h_grouped = work.tile([P, GROUPS * P * PACK], BF16, align_bytes=64)
-            nc.scalar.copy(
-                out=h_grouped[:].rearrange("p (g r t) -> p g r t", g=GROUPS, t=PACK),
-                in_=ht[:].rearrange("p g t r -> p g r t"),
-            )
-            hq_of[i] = quantise(h_grouped, "hq")
+                    nc.tensor.transpose(
+                        out=ht[:, t, :], in_=h_of[i][:, g, t, :], identity=ident_bf16[:]
+                    )
+                h_grouped = halves.tile([P, P, PACK], BF16, align_bytes=64)
+                nc.scalar.copy(out=h_grouped[:], in_=ht[:].rearrange("p t r -> p r t"))
+                hq_words = halves.tile([P, P], U32, align_bytes=64)
+                hq_scales = halves.tile([P, P], U8, align_bytes=64)
+                nc.vector.quantize_mx(
+                    out=hq_words[:].bitcast(FP8X4),
+                    scales=hq_scales[:],
+                    in_=h_grouped[:].rearrange("p r t -> p (r t)"),
+                )
+                hq_of[i].append((hq_words[:], hq_scales[:]))
 
         def project(i):
-            o = [psum_mm.tile([P, BANK], F32, name="o%d" % n, tag="o") for n in range(GROUPS)]
-            mx_product(o, hq_of[i], wo_words, GROUPS)
+            o_of[i] = [psum_o.tile([P, BANK], F32, name="o%d" % n, tag="o") for n in range(GROUPS)]
+            for g in range(GROUPS):
+                for n in range(GROUPS):
+                    mx_pass(o_of[i][n], hq_of[i], wo_words, GROUPS, g, n)
+
+        def add_bo_and_store(i):
             for n in range(GROUPS):
-                result = ahead.tile([P, BANK], F32)
-                nc.vector.tensor_tensor(out=result[:], in0=o[n][:], in1=bo_all[:, n], op=ALU.add)
+                result = halves.tile([P, BANK], F32)
+                nc.vector.tensor_tensor(
+                    out=result[:], in0=o_of[i][n][:], in1=bo_all[:, n], op=ALU.add
+                )
                 nc.sync.dma_start(out=out_rows[:, i, n * BANK : (n + 1) * BANK], in_=result[:])
 
-        norm(0)
+        def each(step, i):
+            if 0 <= i < TILES:
+                step(i)
+
+        statistics(0)
+        scale_and_shift(0)
+        statistics(1)
         transpose_x(0)
-        norm(1)
-        for r in range(TILES + 1):
-            if r >= 1:
-                transpose_h(r - 1)
-            if r + 1 < TILES:
-                transpose_x(r + 1)
-            if r < TILES:
-                gate_times_cat(r)
-            if r >= 1:
-                project(r - 1)
-            if r + 2 < TILES:
-                norm(r + 2)
+        spread_biases()
+        for r in range(TILES + 2):
+            each(product, r - 1)
+            each(scale_and_shift, r + 1)
+            each(transpose_h, r - 2)
+            each(transpose_x, r + 1)
+            each(gate_matmul, r)
+            each(project, r - 2)
+            each(normalise, r)
+            each(silu, r)
+            each(add_bo_and_store, r - 2)
+            each(statistics, r + 2)

@@ -251,7 +251,7 @@ def tile_gatedmultiscaleretentionlayer_pa_kernel(
         def product(i):
             h = work.tile([P, GROUPS, PACK, P], BF16)
             for n in range(GROUPS):
-                nc.gpsimd.tensor_tensor(
+                nc.vector.tensor_tensor(
                     out=h[:, n], in0=gate_of[i][:, n], in1=cat_of[i][:, n], op=ALU.mult
                 )
             h_of[i] = h
@@ -299,11 +299,11 @@ def tile_gatedmultiscaleretentionlayer_pa_kernel(
         transpose_x(0)
         spread_biases()
         for r in range(TILES + 2):
-            each(product, r - 1)
             each(scale_and_shift, r + 1)
             each(transpose_h, r - 2)
             each(transpose_x, r + 1)
             each(gate_matmul, r)
+            each(product, r - 1)
             each(project, r - 2)
             each(normalise, r)
             each(silu, r)

@@ -43,10 +43,8 @@ def tile_gatedmultiscaleretentionlayer_pa_kernel(
         small = stack.enter_context(tc.tile_pool(name="small", bufs=3))
         work = stack.enter_context(tc.tile_pool(name="work", bufs=2))
         halves = stack.enter_context(tc.tile_pool(name="halves", bufs=4))
-        psum_xt = stack.enter_context(tc.psum_pool(name="psum_xt", bufs=1))
-        psum_ht = stack.enter_context(tc.psum_pool(name="psum_ht", bufs=2))
-        psum_z = stack.enter_context(tc.psum_pool(name="psum_z", bufs=3))
-        psum_o = stack.enter_context(tc.psum_pool(name="psum_o", bufs=2))
+        psum_one = stack.enter_context(tc.psum_pool(name="psum_one", bufs=1))
+        psum_two = stack.enter_context(tc.psum_pool(name="psum_two", bufs=2))
         stack.enter_context(tc.manual_schedule())
 
         planes = const.tile([P, WIDTH], U8, align_bytes=64)
@@ -98,46 +96,40 @@ def tile_gatedmultiscaleretentionlayer_pa_kernel(
 
         ident_f32 = const.tile([P, P], F32)
         make_identity(nc, ident_f32[:])
+        ident_bf16 = const.tile([P, P], BF16)
+        make_identity(nc, ident_bf16[:])
 
-        bias_rows = const.tile([P, 2 * WIDTH], BF16)
-        nc.vector.memset(bias_rows[:].bitcast(I32), 0)
-        nc.gpsimd.dma_start(out=bias_rows[0:1, 0:WIDTH], in_=bg.unsqueeze(0))
-        nc.gpsimd.dma_start(out=bias_rows[0:1, WIDTH : 2 * WIDTH], in_=bo.unsqueeze(0))
+        bg_rows = const.tile([P, P], BF16)
+        nc.vector.memset(bg_rows[:].bitcast(I32), 0)
+        nc.gpsimd.dma_start(out=bg_rows[0:HEADS, :], in_=bg.rearrange("(j m) -> j m", m=HEAD))
+        bo_row = const.tile([P, WIDTH], BF16)
+        nc.vector.memset(bo_row[:].bitcast(I32), 0)
+        nc.gpsimd.dma_start(out=bo_row[0:1, :], in_=bo.unsqueeze(0))
         ones = const.tile([P, P], BF16)
         nc.vector.memset(ones[:], 1.0)
         minus_half = const.tile([P, HEADS], F32)
         nc.vector.memset(minus_half[:], -0.5)
 
-        ident_bf16 = const.tile([P, P], BF16)
-        make_identity(nc, ident_bf16[:])
-
         warm = const.tile([P, 1], F32)
         nc.scalar.activation(out=warm[:], in_=minus_half[:, 0:1], func=ACT.Silu)
 
-        bg_sorted = const.tile([P, GROUPS, PACK, P], F32)
+        bg_columns = const.tile([P, HEADS], F32)
         bo_all = const.tile([P, GROUPS, BANK], F32)
 
         def spread_biases():
-            for g in range(GROUPS):
-                spread_bg = psum_z.tile([P, BANK], F32, tag="z")
+            bg_turned = psum_one.tile([P, P], BF16, tag="ht")
+            nc.tensor.transpose(out=bg_turned[:], in_=bg_rows[:], identity=ident_bf16[:])
+            nc.scalar.copy(out=bg_columns[:], in_=bg_turned[:, 0:HEADS])
+            for n in range(GROUPS):
+                spread_bo = psum_two.tile([P, BANK], F32, tag="o")
                 nc.tensor.matmul(
-                    out=spread_bg[:], lhsT=ones[:], rhs=bias_rows[:, g * BANK : (g + 1) * BANK],
+                    out=spread_bo[:], lhsT=ones[:], rhs=bo_row[:, n * BANK : (n + 1) * BANK],
                     start=True, stop=True,
                 )
-                nc.scalar.copy(
-                    out=bg_sorted[:, g], in_=spread_bg[:].rearrange("p (c t) -> p t c", t=PACK)
-                )
-            for g in range(GROUPS):
-                spread_bo = psum_o.tile([P, BANK], F32, tag="o")
-                nc.tensor.matmul(
-                    out=spread_bo[:], lhsT=ones[:],
-                    rhs=bias_rows[:, WIDTH + g * BANK : WIDTH + (g + 1) * BANK],
-                    start=True, stop=True,
-                )
-                nc.vector.tensor_copy(out=bo_all[:, g], in_=spread_bo[:])
+                nc.vector.tensor_copy(out=bo_all[:, n], in_=spread_bo[:])
 
         moments_of, affine_of, cat_of = {}, {}, {}
-        xq_of, z_of, biased_of, gate_of, h_of, hq_of, o_of = {}, {}, {}, {}, {}, {}, {}
+        xq_of, zt_of, gate_t_of, gate_of, h_of, hq_of, o_of = {}, {}, {}, {}, {}, {}, {}
 
         def statistics(i):
             stats = small.tile([P, HEADS, 6], F32)
@@ -149,23 +141,23 @@ def tile_gatedmultiscaleretentionlayer_pa_kernel(
             mean_odd, m2_odd = stats[:, :, 4], stats[:, :, 5]
             gap = small.tile([P, HEADS], F32)
             nc.vector.tensor_tensor(out=gap[:], in0=mean_even, in1=mean_odd, op=ALU.subtract)
-            gap_sq = small.tile([P, HEADS], F32)
-            nc.vector.scalar_tensor_tensor(
-                out=gap_sq[:], in0=gap[:], scalar=0.25, in1=gap[:], op0=ALU.mult, op1=ALU.mult
-            )
             m2 = small.tile([P, HEADS], F32)
             nc.vector.scalar_tensor_tensor(
                 out=m2[:], in0=m2_even, scalar=HEAD * EPS, in1=m2_odd, op0=ALU.add, op1=ALU.add
             )
-            var_eps = small.tile([P, HEADS], F32)
+            gap_sq = small.tile([P, HEADS], F32)
             nc.vector.scalar_tensor_tensor(
-                out=var_eps[:], in0=m2[:], scalar=1.0 / HEAD, in1=gap_sq[:],
-                op0=ALU.mult, op1=ALU.add,
+                out=gap_sq[:], in0=gap[:], scalar=0.25, in1=gap[:], op0=ALU.mult, op1=ALU.mult
             )
             minus_mean = small.tile([P, HEADS], F32)
             nc.vector.scalar_tensor_tensor(
                 out=minus_mean[:], in0=gap[:], scalar=-0.5, in1=mean_odd,
                 op0=ALU.mult, op1=ALU.subtract,
+            )
+            var_eps = small.tile([P, HEADS], F32)
+            nc.vector.scalar_tensor_tensor(
+                out=var_eps[:], in0=m2[:], scalar=1.0 / HEAD, in1=gap_sq[:],
+                op0=ALU.mult, op1=ALU.add,
             )
             moments_of[i] = (var_eps, minus_mean)
 
@@ -196,7 +188,7 @@ def tile_gatedmultiscaleretentionlayer_pa_kernel(
         def transpose_x(i):
             x_words = x_sb[i][:].bitcast(F32)
             pairs = K_PASS // 2
-            xt = psum_xt.tile([P, GROUPS, 2, P], F32)
+            xt = psum_one.tile([P, GROUPS, 2, P], F32)
             for g in range(GROUPS):
                 for u in range(2):
                     nc.tensor.transpose(
@@ -216,56 +208,72 @@ def tile_gatedmultiscaleretentionlayer_pa_kernel(
                 scales=xq_scales[:].rearrange("p g r -> p (g r)"),
                 in_=x_grouped[:],
             )
-            xq_of[i] = [(xq_words[:, g, :], xq_scales[:, g, :]) for g in range(GROUPS)]
-
-        def mx_pass(bank, lhs, weight_words, first_plane, g, n):
-            words, scales = lhs[g]
-            nc.tensor.matmul_mx(
-                out=bank[:],
-                lhsT=words.bitcast(FP8X4),
-                lhsT_scale=scales,
-                rhs=weight_words[:, g, n * BANK : (n + 1) * BANK].bitcast(FP8X4),
-                rhs_scale=planes[PACK * (first_plane + g) : P, n * BANK : (n + 1) * BANK],
-                start=(g == 0),
-                stop=(g == GROUPS - 1),
-            )
+            xq_of[i] = (xq_words, xq_scales)
 
         def gate_matmul(i):
-            biased = work.tile([P, GROUPS, PACK, P], F32)
+            xq_words, xq_scales = xq_of[i]
+            zt_of[i] = []
             for n in range(GROUPS):
-                z = psum_z.tile([P, BANK], F32, tag="z")
-                for g in range(GROUPS):
-                    mx_pass(z, xq_of[i], wg_words, 0, g, n)
-                nc.vector.tensor_tensor(
-                    out=biased[:, n], in0=z[:].rearrange("p (c t) -> p t c", t=PACK),
-                    in1=bg_sorted[:, n], op=ALU.add,
-                )
-            biased_of[i] = biased
+                zt = psum_two.tile([P, HEADS_PER_GROUP, P], F32)
+                for j in range(HEADS_PER_GROUP):
+                    head = n * HEADS_PER_GROUP + j
+                    columns = slice(head * HEAD, (head + 1) * HEAD)
+                    for g in range(GROUPS):
+                        nc.tensor.matmul_mx(
+                            out=zt[:, j, :],
+                            lhsT=wg_words[:, g, columns].bitcast(FP8X4),
+                            lhsT_scale=planes[PACK * g : P, columns],
+                            rhs=xq_words[:, g, :].bitcast(FP8X4),
+                            rhs_scale=xq_scales[:, g, :],
+                            start=(g == 0),
+                            stop=(g == GROUPS - 1),
+                        )
+                zt_of[i].append(zt)
 
         def silu(i):
-            gate = work.tile([P, GROUPS, PACK, P], F32)
+            gate_t = work.tile([P, HEADS, P], F32)
+            for head in range(HEADS):
+                n, j = divmod(head, HEADS_PER_GROUP)
+                nc.scalar.activation(
+                    out=gate_t[:, head, :], in_=zt_of[i][n][:, j, :], func=ACT.Silu,
+                    bias=bg_columns[:, head : head + 1],
+                )
+            gate_t_of[i] = gate_t
+
+        def transpose_gate(i):
+            gate_of[i] = []
             for n in range(GROUPS):
-                nc.scalar.activation(out=gate[:, n], in_=biased_of[i][:, n], func=ACT.Silu)
-            gate_of[i] = gate
+                gate = psum_two.tile([P, BANK], F32)
+                for j in range(HEADS_PER_GROUP):
+                    nc.tensor.transpose(
+                        out=gate[:, j * HEAD : (j + 1) * HEAD],
+                        in_=gate_t_of[i][:, n * HEADS_PER_GROUP + j, :],
+                        identity=ident_f32[:],
+                    )
+                gate_of[i].append(gate)
 
         def product(i):
             h = work.tile([P, GROUPS, PACK, P], BF16)
             for n in range(GROUPS):
                 nc.vector.tensor_tensor(
-                    out=h[:, n], in0=gate_of[i][:, n], in1=cat_of[i][:, n], op=ALU.mult
+                    out=h[:, n],
+                    in0=gate_of[i][n][:].rearrange("p (c t) -> p t c", t=PACK),
+                    in1=cat_of[i][:, n],
+                    op=ALU.mult,
                 )
             h_of[i] = h
 
         def transpose_h(i):
-            hq_of[i] = []
+            ht = psum_one.tile([P, GROUPS, PACK, P], BF16)
             for g in range(GROUPS):
-                ht = psum_ht.tile([P, PACK, P], BF16)
                 for t in range(PACK):
                     nc.tensor.transpose(
-                        out=ht[:, t, :], in_=h_of[i][:, g, t, :], identity=ident_bf16[:]
+                        out=ht[:, g, t, :], in_=h_of[i][:, g, t, :], identity=ident_bf16[:]
                     )
+            hq_of[i] = []
+            for g in range(GROUPS):
                 h_grouped = halves.tile([P, P, PACK], BF16, align_bytes=64)
-                nc.scalar.copy(out=h_grouped[:], in_=ht[:].rearrange("p t r -> p r t"))
+                nc.scalar.copy(out=h_grouped[:], in_=ht[:, g].rearrange("p t r -> p r t"))
                 hq_words = halves.tile([P, P], U32, align_bytes=64)
                 hq_scales = halves.tile([P, P], U8, align_bytes=64)
                 nc.vector.quantize_mx(
@@ -273,13 +281,22 @@ def tile_gatedmultiscaleretentionlayer_pa_kernel(
                     scales=hq_scales[:],
                     in_=h_grouped[:].rearrange("p r t -> p (r t)"),
                 )
-                hq_of[i].append((hq_words[:], hq_scales[:]))
+                hq_of[i].append((hq_words, hq_scales))
 
         def project(i):
-            o_of[i] = [psum_o.tile([P, BANK], F32, name="o%d" % n, tag="o") for n in range(GROUPS)]
+            o_of[i] = [psum_two.tile([P, BANK], F32, name="o%d" % n, tag="o") for n in range(GROUPS)]
             for g in range(GROUPS):
+                hq_words, hq_scales = hq_of[i][g]
                 for n in range(GROUPS):
-                    mx_pass(o_of[i][n], hq_of[i], wo_words, GROUPS, g, n)
+                    nc.tensor.matmul_mx(
+                        out=o_of[i][n][:],
+                        lhsT=hq_words[:].bitcast(FP8X4),
+                        lhsT_scale=hq_scales[:],
+                        rhs=wo_words[:, g, n * BANK : (n + 1) * BANK].bitcast(FP8X4),
+                        rhs_scale=planes[PACK * (GROUPS + g) : P, n * BANK : (n + 1) * BANK],
+                        start=(g == 0),
+                        stop=(g == GROUPS - 1),
+                    )
 
         def add_bo_and_store(i):
             for n in range(GROUPS):
@@ -301,11 +318,12 @@ def tile_gatedmultiscaleretentionlayer_pa_kernel(
         for r in range(TILES + 2):
             each(scale_and_shift, r + 1)
             each(transpose_h, r - 2)
+            each(transpose_gate, r - 1)
             each(transpose_x, r + 1)
-            each(gate_matmul, r)
             each(product, r - 1)
+            each(gate_matmul, r)
             each(project, r - 2)
-            each(normalise, r)
             each(silu, r)
-            each(add_bo_and_store, r - 2)
+            each(normalise, r)
             each(statistics, r + 2)
+            each(add_bo_and_store, r - 2)

@@ -318,10 +318,10 @@ def tile_gatedmultiscaleretentionlayer_pa_kernel(
         for r in range(TILES + 2):
             each(scale_and_shift, r + 1)
             each(transpose_h, r - 2)
-            each(transpose_gate, r - 1)
             each(transpose_x, r + 1)
-            each(product, r - 1)
             each(gate_matmul, r)
+            each(transpose_gate, r - 1)
+            each(product, r - 1)
             each(project, r - 2)
             each(silu, r)
             each(normalise, r)

@@ -128,7 +128,7 @@ def tile_gatedmultiscaleretentionlayer_pa_kernel(
                 )
                 nc.vector.tensor_copy(out=bo_all[:, n], in_=spread_bo[:])
 
-        moments_of, affine_of, cat_of = {}, {}, {}
+        stats_of, joined_of, affine_of, cat_of = {}, {}, {}, {}
         xq_of, zt_of, gate_t_of, gate_of, h_of, hq_of, o_of = {}, {}, {}, {}, {}, {}, {}
 
         def statistics(i):
@@ -137,6 +137,10 @@ def tile_gatedmultiscaleretentionlayer_pa_kernel(
                 nc.vector.bn_stats(
                     out=stats[:, head, :], in_=ret_sb[i][:, head * HEAD : (head + 1) * HEAD]
                 )
+            stats_of[i] = stats
+
+        def join_halves(i):
+            stats = stats_of[i]
             mean_even, m2_even = stats[:, :, 1], stats[:, :, 2]
             mean_odd, m2_odd = stats[:, :, 4], stats[:, :, 5]
             gap = small.tile([P, HEADS], F32)
@@ -145,28 +149,33 @@ def tile_gatedmultiscaleretentionlayer_pa_kernel(
             nc.vector.scalar_tensor_tensor(
                 out=m2[:], in0=m2_even, scalar=HEAD * EPS, in1=m2_odd, op0=ALU.add, op1=ALU.add
             )
-            gap_sq = small.tile([P, HEADS], F32)
+            minus_mean2 = small.tile([P, HEADS], F32)
             nc.vector.scalar_tensor_tensor(
-                out=gap_sq[:], in0=gap[:], scalar=0.25, in1=gap[:], op0=ALU.mult, op1=ALU.mult
-            )
-            minus_mean = small.tile([P, HEADS], F32)
-            nc.vector.scalar_tensor_tensor(
-                out=minus_mean[:], in0=gap[:], scalar=-0.5, in1=mean_odd,
+                out=minus_mean2[:], in0=mean_even, scalar=-1.0, in1=mean_odd,
                 op0=ALU.mult, op1=ALU.subtract,
             )
-            var_eps = small.tile([P, HEADS], F32)
-            nc.vector.scalar_tensor_tensor(
-                out=var_eps[:], in0=m2[:], scalar=1.0 / HEAD, in1=gap_sq[:],
-                op0=ALU.mult, op1=ALU.add,
-            )
-            moments_of[i] = (var_eps, minus_mean)
+            joined_of[i] = (gap, m2, minus_mean2)
 
         def scale_and_shift(i):
-            var_eps, minus_mean = moments_of[i]
+            gap, m2, minus_mean2 = joined_of[i]
+            gap_sq = small.tile([P, HEADS], F32)
+            nc.gpsimd.tensor_tensor(out=gap_sq[:], in0=gap[:], in1=gap[:], op=ALU.mult)
+            within = small.tile([P, HEADS], F32)
+            nc.gpsimd.tensor_scalar(
+                out=within[:], in0=m2[:], scalar1=4.0 / HEAD, scalar2=0.0, op0=ALU.mult, op1=ALU.add
+            )
+            var4 = small.tile([P, HEADS], F32)
+            nc.gpsimd.tensor_tensor(out=var4[:], in0=gap_sq[:], in1=within[:], op=ALU.add)
+            half_rstd = small.tile([P, HEADS], F32)
+            nc.gpsimd.tensor_tensor(out=half_rstd[:], in0=var4[:], in1=minus_half[:], op=ALU.pow)
             rstd = small.tile([P, HEADS], F32)
-            nc.gpsimd.tensor_tensor(out=rstd[:], in0=var_eps[:], in1=minus_half[:], op=ALU.pow)
+            nc.gpsimd.tensor_scalar(
+                out=rstd[:], in0=half_rstd[:], scalar1=2.0, scalar2=0.0, op0=ALU.mult, op1=ALU.add
+            )
             shift = small.tile([P, HEADS], F32)
-            nc.gpsimd.tensor_tensor(out=shift[:], in0=minus_mean[:], in1=rstd[:], op=ALU.mult)
+            nc.gpsimd.tensor_tensor(
+                out=shift[:], in0=minus_mean2[:], in1=half_rstd[:], op=ALU.mult
+            )
             affine_of[i] = (rstd, shift)
 
         def normalise(i):
@@ -311,8 +320,10 @@ def tile_gatedmultiscaleretentionlayer_pa_kernel(
                 step(i)
 
         statistics(0)
-        scale_and_shift(0)
         statistics(1)
+        join_halves(0)
+        scale_and_shift(0)
+        join_halves(1)
         transpose_x(0)
         spread_biases()
         for r in range(TILES + 2):
@@ -327,3 +338,4 @@ def tile_gatedmultiscaleretentionlayer_pa_kernel(
             each(normalise, r)
             each(statistics, r + 2)
             each(add_bo_and_store, r - 2)
+            each(join_halves, r + 2)

@@ -40,19 +40,23 @@ def tile_gatedmultiscaleretentionlayer_pa_kernel(
 
     with ExitStack() as stack:
         const = stack.enter_context(tc.tile_pool(name="const", bufs=1))
-        small = stack.enter_context(tc.tile_pool(name="small", bufs=3))
-        work = stack.enter_context(tc.tile_pool(name="work", bufs=2))
+        small = stack.enter_context(tc.tile_pool(name="small", bufs=4))
+        work = stack.enter_context(tc.tile_pool(name="work", bufs=3))
         halves = stack.enter_context(tc.tile_pool(name="halves", bufs=4))
-        psum_one = stack.enter_context(tc.psum_pool(name="psum_one", bufs=1))
-        psum_two = stack.enter_context(tc.psum_pool(name="psum_two", bufs=2))
+        psum_x = stack.enter_context(tc.psum_pool(name="psum_x", bufs=1))
+        psum_z = stack.enter_context(tc.psum_pool(name="psum_z", bufs=2))
+        psum_c = stack.enter_context(tc.psum_pool(name="psum_c", bufs=3))
+        psum_o = stack.enter_context(tc.psum_pool(name="psum_o", bufs=2))
         stack.enter_context(tc.manual_schedule())
 
-        planes = const.tile([P, WIDTH], U8, align_bytes=64)
-        nc.vector.memset(planes[:].bitcast(I32), 0)
+        wg_planes_raw = const.tile([P, WIDTH], U8, align_bytes=64)
+        nc.vector.memset(wg_planes_raw[:].bitcast(I32), 0)
+        wo_planes = const.tile([P, WIDTH], U8, align_bytes=64)
+        nc.vector.memset(wo_planes[:].bitcast(I32), 0)
 
         x_sb = [const.tile([P, WIDTH], BF16, name="x%d" % i) for i in range(TILES)]
         ret_sb = [const.tile([P, WIDTH], BF16, name="ret%d" % i) for i in range(TILES)]
-        wg_words = const.tile([P, GROUPS, WIDTH], U32, align_bytes=64)
+        wg_raw = const.tile([P, GROUPS, WIDTH], U32, align_bytes=64)
         wo_words = const.tile([P, GROUPS, WIDTH], U32, align_bytes=64)
 
         def load_x(i):
@@ -61,9 +65,9 @@ def tile_gatedmultiscaleretentionlayer_pa_kernel(
         def load_ret(i):
             nc.sync.dma_start(out=ret_sb[i][:], in_=ret_rows[:, i, :])
 
-        def load_scales(scales, first_plane):
+        def load_scales(planes, scales):
             for quadrant in range(4):
-                top = 32 * quadrant + PACK * first_plane
+                top = 32 * quadrant
                 nc.sync.dma_start(
                     out=planes[top : top + PACK * GROUPS, :].bitcast(I32),
                     in_=scales[:, 4 * quadrant : 4 * quadrant + 4, :].bitcast(I32),
@@ -80,102 +84,93 @@ def tile_gatedmultiscaleretentionlayer_pa_kernel(
 
         load_ret(0)
         load_x(0)
-        load_ret(1)
-        load_scales(Wg_scales, 0)
-        load_words(wg_words, Wg_words, 0)
+        load_scales(wg_planes_raw, Wg_scales)
+        load_words(wg_raw, Wg_words, 0)
+        load_words(wg_raw, Wg_words, 1)
         load_x(1)
-        load_words(wg_words, Wg_words, 1)
+        load_ret(1)
         load_ret(2)
         load_x(2)
-        load_scales(Wo_scales, GROUPS)
+        load_ret(3)
+        load_scales(wo_planes, Wo_scales)
         load_words(wo_words, Wo_words, 0)
         load_words(wo_words, Wo_words, 1)
         for i in range(3, TILES):
-            load_ret(i)
             load_x(i)
+            if i + 1 < TILES:
+                load_ret(i + 1)
 
-        ident_f32 = const.tile([P, P], F32)
-        make_identity(nc, ident_f32[:])
-        ident_bf16 = const.tile([P, P], BF16)
-        make_identity(nc, ident_bf16[:])
-
-        bg_rows = const.tile([P, P], BF16)
-        nc.vector.memset(bg_rows[:].bitcast(I32), 0)
-        nc.gpsimd.dma_start(out=bg_rows[0:HEADS, :], in_=bg.rearrange("(j m) -> j m", m=HEAD))
-        bo_row = const.tile([P, WIDTH], BF16)
-        nc.vector.memset(bo_row[:].bitcast(I32), 0)
-        nc.gpsimd.dma_start(out=bo_row[0:1, :], in_=bo.unsqueeze(0))
-        ones = const.tile([P, P], BF16)
-        nc.vector.memset(ones[:], 1.0)
+        ident = const.tile([P, P], F32)
+        make_identity(nc, ident[:])
         minus_half = const.tile([P, HEADS], F32)
-        nc.vector.memset(minus_half[:], -0.5)
+        nc.gpsimd.memset(minus_half[:], -0.5)
 
         warm = const.tile([P, 1], F32)
         nc.scalar.activation(out=warm[:], in_=minus_half[:, 0:1], func=ACT.Silu)
 
-        bg_columns = const.tile([P, HEADS], F32)
+        bg_bf16 = const.tile([P, GROUPS, PACK], BF16)
+        nc.gpsimd.dma_start(
+            out=bg_bf16[:], in_=bg.rearrange("(g p t) -> p g t", g=GROUPS, t=PACK)
+        )
+        bg_columns = const.tile([P, GROUPS, PACK], F32)
+        bo_row = const.tile([P, WIDTH], BF16)
+        nc.gpsimd.memset(bo_row[:].bitcast(I32), 0)
+        nc.gpsimd.dma_start(out=bo_row[0:1, :], in_=bo.unsqueeze(0))
+        ones = const.tile([P, P], BF16)
+        nc.gpsimd.memset(ones[:], 1.0)
+        nc.gpsimd.tensor_copy(out=bg_columns[:], in_=bg_bf16[:])
         bo_all = const.tile([P, GROUPS, BANK], F32)
 
-        def spread_biases():
-            bg_turned = psum_one.tile([P, P], BF16, tag="ht")
-            nc.tensor.transpose(out=bg_turned[:], in_=bg_rows[:], identity=ident_bf16[:])
-            nc.scalar.copy(out=bg_columns[:], in_=bg_turned[:, 0:HEADS])
+        def spread_bo():
             for n in range(GROUPS):
-                spread_bo = psum_two.tile([P, BANK], F32, tag="o")
+                spread = psum_o.tile([P, BANK], F32, tag="o")
                 nc.tensor.matmul(
-                    out=spread_bo[:], lhsT=ones[:], rhs=bo_row[:, n * BANK : (n + 1) * BANK],
+                    out=spread[:], lhsT=ones[:], rhs=bo_row[:, n * BANK : (n + 1) * BANK],
                     start=True, stop=True,
                 )
-                nc.vector.tensor_copy(out=bo_all[:, n], in_=spread_bo[:])
+                nc.scalar.copy(out=bo_all[:, n], in_=spread[:])
 
-        stats_of, joined_of, affine_of, cat_of = {}, {}, {}, {}
-        xq_of, zt_of, gate_t_of, gate_of, h_of, hq_of, o_of = {}, {}, {}, {}, {}, {}, {}
+        wg_words = const.tile([P, GROUPS, WIDTH], U32, align_bytes=64)
+        wg_planes = const.tile([P, WIDTH], U8, align_bytes=64)
+
+        def sort_columns(n):
+            columns = slice(n * BANK, (n + 1) * BANK)
+            nc.vector.tensor_copy(
+                out=wg_planes[:, columns].rearrange("p (t m) -> p t m", t=PACK),
+                in_=wg_planes_raw[:, columns].rearrange("p (m t) -> p t m", t=PACK),
+            )
+            for g in range(GROUPS):
+                nc.vector.tensor_copy(
+                    out=wg_words[:, g, columns].bitcast(I32).rearrange("p (t m) -> p t m", t=PACK),
+                    in_=wg_raw[:, g, columns].bitcast(I32).rearrange("p (m t) -> p t m", t=PACK),
+                )
+
+        affine_of, cat_of, ct_of = {}, {}, {}
+        xt_of, xg_of, xq_of, zt_of, gate_of, h_of, hq_of, o_of = {}, {}, {}, {}, {}, {}, {}, {}
 
         def statistics(i):
-            stats = small.tile([P, HEADS, 6], F32)
-            for head in range(HEADS):
+            stats = small.tile([P, HEADS // 2, 6], F32)
+            for pair in range(HEADS // 2):
                 nc.vector.bn_stats(
-                    out=stats[:, head, :], in_=ret_sb[i][:, head * HEAD : (head + 1) * HEAD]
+                    out=stats[:, pair, :],
+                    in_=ret_sb[i][:, 2 * pair * HEAD : 2 * (pair + 1) * HEAD].rearrange(
+                        "p (h c) -> p c h", h=2
+                    ),
                 )
-            stats_of[i] = stats
-
-        def join_halves(i):
-            stats = stats_of[i]
-            mean_even, m2_even = stats[:, :, 1], stats[:, :, 2]
-            mean_odd, m2_odd = stats[:, :, 4], stats[:, :, 5]
-            gap = small.tile([P, HEADS], F32)
-            nc.vector.tensor_tensor(out=gap[:], in0=mean_even, in1=mean_odd, op=ALU.subtract)
-            m2 = small.tile([P, HEADS], F32)
-            nc.vector.scalar_tensor_tensor(
-                out=m2[:], in0=m2_even, scalar=HEAD * EPS, in1=m2_odd, op0=ALU.add, op1=ALU.add
-            )
-            minus_mean2 = small.tile([P, HEADS], F32)
-            nc.vector.scalar_tensor_tensor(
-                out=minus_mean2[:], in0=mean_even, scalar=-1.0, in1=mean_odd,
-                op0=ALU.mult, op1=ALU.subtract,
-            )
-            joined_of[i] = (gap, m2, minus_mean2)
-
-        def scale_and_shift(i):
-            gap, m2, minus_mean2 = joined_of[i]
-            gap_sq = small.tile([P, HEADS], F32)
-            nc.gpsimd.tensor_tensor(out=gap_sq[:], in0=gap[:], in1=gap[:], op=ALU.mult)
-            within = small.tile([P, HEADS], F32)
+            by_head = stats[:].rearrange("p k (e s) -> p (k e) s", e=2)
+            mean, m2 = by_head[:, :, 1], by_head[:, :, 2]
+            var = small.tile([P, HEADS], F32)
             nc.gpsimd.tensor_scalar(
-                out=within[:], in0=m2[:], scalar1=4.0 / HEAD, scalar2=0.0, op0=ALU.mult, op1=ALU.add
+                out=var[:], in0=m2, scalar1=1.0 / HEAD, scalar2=EPS, op0=ALU.mult, op1=ALU.add
             )
-            var4 = small.tile([P, HEADS], F32)
-            nc.gpsimd.tensor_tensor(out=var4[:], in0=gap_sq[:], in1=within[:], op=ALU.add)
-            half_rstd = small.tile([P, HEADS], F32)
-            nc.gpsimd.tensor_tensor(out=half_rstd[:], in0=var4[:], in1=minus_half[:], op=ALU.pow)
+            minus_mean = small.tile([P, HEADS], F32)
+            nc.gpsimd.tensor_scalar(
+                out=minus_mean[:], in0=mean, scalar1=-1.0, scalar2=0.0, op0=ALU.mult, op1=ALU.add
+            )
             rstd = small.tile([P, HEADS], F32)
-            nc.gpsimd.tensor_scalar(
-                out=rstd[:], in0=half_rstd[:], scalar1=2.0, scalar2=0.0, op0=ALU.mult, op1=ALU.add
-            )
+            nc.gpsimd.tensor_tensor(out=rstd[:], in0=var[:], in1=minus_half[:], op=ALU.pow)
             shift = small.tile([P, HEADS], F32)
-            nc.gpsimd.tensor_tensor(
-                out=shift[:], in0=minus_mean2[:], in1=half_rstd[:], op=ALU.mult
-            )
+            nc.gpsimd.tensor_tensor(out=shift[:], in0=minus_mean[:], in1=rstd[:], op=ALU.mult)
             affine_of[i] = (rstd, shift)
 
         def normalise(i):
@@ -194,106 +189,110 @@ def tile_gatedmultiscaleretentionlayer_pa_kernel(
                 )
             cat_of[i] = cat
 
+        def transpose_cat(i):
+            ct_of[i] = []
+            for g in range(GROUPS):
+                ct = psum_c.tile([P, PACK, P], F32, tag="ct")
+                for t in range(PACK):
+                    nc.tensor.transpose(
+                        out=ct[:, t, :], in_=cat_of[i][:, g, t, :], identity=ident[:]
+                    )
+                ct_of[i].append(ct)
+
         def transpose_x(i):
             x_words = x_sb[i][:].bitcast(F32)
             pairs = K_PASS // 2
-            xt = psum_one.tile([P, GROUPS, 2, P], F32)
+            xt = psum_x.tile([P, GROUPS, 2, P], F32)
             for g in range(GROUPS):
                 for u in range(2):
                     nc.tensor.transpose(
                         out=xt[:, g, u, :],
                         in_=x_words[:, g * pairs + u : (g + 1) * pairs : 2],
-                        identity=ident_f32[:],
+                        identity=ident[:],
                     )
+            xt_of[i] = xt
+
+        def group_x(i):
             x_grouped = work.tile([P, GROUPS * P * PACK], BF16, align_bytes=64)
             nc.scalar.copy(
                 out=x_grouped[:].bitcast(F32).rearrange("p (g r u) -> p g r u", g=GROUPS, u=2),
-                in_=xt[:].rearrange("p g u r -> p g r u"),
+                in_=xt_of[i][:].rearrange("p g u r -> p g r u"),
             )
+            xg_of[i] = x_grouped
+
+        def quantise_x(i):
             xq_words = work.tile([P, GROUPS, P], U32, align_bytes=64)
             xq_scales = work.tile([P, GROUPS, P], U8, align_bytes=64)
             nc.vector.quantize_mx(
                 out=xq_words[:].rearrange("p g r -> p (g r)").bitcast(FP8X4),
                 scales=xq_scales[:].rearrange("p g r -> p (g r)"),
-                in_=x_grouped[:],
+                in_=xg_of[i][:],
             )
             xq_of[i] = (xq_words, xq_scales)
 
-        def gate_matmul(i):
+        def gate_half(i, n):
             xq_words, xq_scales = xq_of[i]
-            zt_of[i] = []
+            zt = psum_z.tile([P, PACK, P], F32)
+            for t in range(PACK):
+                columns = slice(n * BANK + t * P, n * BANK + (t + 1) * P)
+                for g in range(GROUPS):
+                    nc.tensor.matmul_mx(
+                        out=zt[:, t, :],
+                        lhsT=wg_words[:, g, columns].bitcast(FP8X4),
+                        lhsT_scale=wg_planes[PACK * g : P, columns],
+                        rhs=xq_words[:, g, :].bitcast(FP8X4),
+                        rhs_scale=xq_scales[:, g, :],
+                        start=(g == 0),
+                        stop=(g == GROUPS - 1),
+                    )
+            zt_of.setdefault(i, []).append(zt)
+
+        def gate_matmul(i):
             for n in range(GROUPS):
-                zt = psum_two.tile([P, HEADS_PER_GROUP, P], F32)
-                for j in range(HEADS_PER_GROUP):
-                    head = n * HEADS_PER_GROUP + j
-                    columns = slice(head * HEAD, (head + 1) * HEAD)
-                    for g in range(GROUPS):
-                        nc.tensor.matmul_mx(
-                            out=zt[:, j, :],
-                            lhsT=wg_words[:, g, columns].bitcast(FP8X4),
-                            lhsT_scale=planes[PACK * g : P, columns],
-                            rhs=xq_words[:, g, :].bitcast(FP8X4),
-                            rhs_scale=xq_scales[:, g, :],
-                            start=(g == 0),
-                            stop=(g == GROUPS - 1),
-                        )
-                zt_of[i].append(zt)
+                gate_half(i, n)
+
+        def silu_half(i, n):
+            gate = halves.tile([P, PACK, P], F32)
+            for t in range(PACK):
+                nc.scalar.activation(
+                    out=gate[:, t, :], in_=zt_of[i][n][:, t, :], func=ACT.Silu,
+                    bias=bg_columns[:, n, t : t + 1],
+                )
+            gate_of.setdefault(i, []).append(gate)
 
         def silu(i):
-            gate_t = work.tile([P, HEADS, P], F32)
-            for head in range(HEADS):
-                n, j = divmod(head, HEADS_PER_GROUP)
-                nc.scalar.activation(
-                    out=gate_t[:, head, :], in_=zt_of[i][n][:, j, :], func=ACT.Silu,
-                    bias=bg_columns[:, head : head + 1],
-                )
-            gate_t_of[i] = gate_t
-
-        def transpose_gate(i):
-            gate_of[i] = []
             for n in range(GROUPS):
-                gate = psum_two.tile([P, BANK], F32)
-                for j in range(HEADS_PER_GROUP):
-                    nc.tensor.transpose(
-                        out=gate[:, j * HEAD : (j + 1) * HEAD],
-                        in_=gate_t_of[i][:, n * HEADS_PER_GROUP + j, :],
-                        identity=ident_f32[:],
-                    )
-                gate_of[i].append(gate)
+                silu_half(i, n)
 
         def product(i):
-            h = work.tile([P, GROUPS, PACK, P], BF16)
-            for n in range(GROUPS):
+            h_of[i] = []
+            for g in range(GROUPS):
+                h = halves.tile([P, P, PACK], BF16, align_bytes=64)
                 nc.vector.tensor_tensor(
-                    out=h[:, n],
-                    in0=gate_of[i][n][:].rearrange("p (c t) -> p t c", t=PACK),
-                    in1=cat_of[i][:, n],
+                    out=h[:],
+                    in0=ct_of[i][g][:].rearrange("p t r -> p r t"),
+                    in1=gate_of[i][g][:].rearrange("p t r -> p r t"),
                     op=ALU.mult,
                 )
-            h_of[i] = h
+                h_of[i].append(h)
 
-        def transpose_h(i):
-            ht = psum_one.tile([P, GROUPS, PACK, P], BF16)
-            for g in range(GROUPS):
-                for t in range(PACK):
-                    nc.tensor.transpose(
-                        out=ht[:, g, t, :], in_=h_of[i][:, g, t, :], identity=ident_bf16[:]
-                    )
+        def quantise_h(i):
             hq_of[i] = []
             for g in range(GROUPS):
-                h_grouped = halves.tile([P, P, PACK], BF16, align_bytes=64)
-                nc.scalar.copy(out=h_grouped[:], in_=ht[:, g].rearrange("p t r -> p r t"))
                 hq_words = halves.tile([P, P], U32, align_bytes=64)
                 hq_scales = halves.tile([P, P], U8, align_bytes=64)
                 nc.vector.quantize_mx(
                     out=hq_words[:].bitcast(FP8X4),
                     scales=hq_scales[:],
-                    in_=h_grouped[:].rearrange("p r t -> p (r t)"),
+                    in_=h_of[i][g][:].rearrange("p r t -> p (r t)"),
                 )
                 hq_of[i].append((hq_words, hq_scales))
 
         def project(i):
-            o_of[i] = [psum_two.tile([P, BANK], F32, name="o%d" % n, tag="o") for n in range(GROUPS)]
+            if i == TILES - 1:
+                o_of[i] = [psum_c.tile([P, BANK], F32, name="o%d" % n, tag="ct") for n in range(GROUPS)]
+            else:
+                o_of[i] = [psum_o.tile([P, BANK], F32, name="o%d" % n, tag="o") for n in range(GROUPS)]
             for g in range(GROUPS):
                 hq_words, hq_scales = hq_of[i][g]
                 for n in range(GROUPS):
@@ -302,7 +301,7 @@ def tile_gatedmultiscaleretentionlayer_pa_kernel(
                         lhsT=hq_words[:].bitcast(FP8X4),
                         lhsT_scale=hq_scales[:],
                         rhs=wo_words[:, g, n * BANK : (n + 1) * BANK].bitcast(FP8X4),
-                        rhs_scale=planes[PACK * (GROUPS + g) : P, n * BANK : (n + 1) * BANK],
+                        rhs_scale=wo_planes[PACK * g : P, n * BANK : (n + 1) * BANK],
                         start=(g == 0),
                         stop=(g == GROUPS - 1),
                     )
@@ -320,22 +319,38 @@ def tile_gatedmultiscaleretentionlayer_pa_kernel(
                 step(i)
 
         statistics(0)
-        statistics(1)
-        join_halves(0)
-        scale_and_shift(0)
-        join_halves(1)
         transpose_x(0)
-        spread_biases()
-        for r in range(TILES + 2):
-            each(scale_and_shift, r + 1)
-            each(transpose_h, r - 2)
-            each(transpose_x, r + 1)
-            each(gate_matmul, r)
-            each(transpose_gate, r - 1)
-            each(product, r - 1)
-            each(project, r - 2)
-            each(silu, r)
-            each(normalise, r)
-            each(statistics, r + 2)
-            each(add_bo_and_store, r - 2)
-            each(join_halves, r + 2)
+        group_x(0)
+        sort_columns(0)
+        quantise_x(0)
+        sort_columns(1)
+        gate_half(0, 0)
+        transpose_x(1)
+        gate_half(0, 1)
+        silu_half(0, 0)
+        group_x(1)
+        normalise(0)
+        silu_half(0, 1)
+        transpose_cat(0)
+        statistics(1)
+        quantise_x(1)
+        transpose_x(2)
+        group_x(2)
+        normalise(1)
+        statistics(2)
+        statistics(3)
+        for r in range(TILES + 1):
+            each(product, r)
+            each(transpose_x, r + 3)
+            each(group_x, r + 3)
+            each(gate_matmul, r + 1)
+            each(silu, r + 1)
+            each(normalise, r + 2)
+            each(project, r - 1)
+            each(transpose_cat, r + 1)
+            each(statistics, r + 4)
+            each(quantise_h, r)
+            each(quantise_x, r + 2)
+            if r == 0:
+                spread_bo()
+            each(add_bo_and_store, r - 1)

@@ -25,6 +25,7 @@ GROUPS = WIDTH // K_PASS
 HEADS_PER_GROUP = HEADS // GROUPS
 QUARTER = HEAD // PACK
 EPS = 1e-5
+RUN = 4
 
 FLOPS = 2 * 2 * TOKENS * WIDTH * WIDTH
 
@@ -269,9 +270,9 @@ def tile_gatedmultiscaleretentionlayer_pa_kernel(
             for g in range(GROUPS):
                 h = halves.tile([P, P, PACK], BF16, align_bytes=64)
                 nc.vector.tensor_tensor(
-                    out=h[:],
-                    in0=ct_of[i][g][:].rearrange("p t r -> p r t"),
-                    in1=gate_of[i][g][:].rearrange("p t r -> p r t"),
+                    out=h[:].rearrange("p (c k) t -> p c t k", k=RUN),
+                    in0=ct_of[i][g][:].rearrange("p t (c k) -> p c t k", k=RUN),
+                    in1=gate_of[i][g][:].rearrange("p t (c k) -> p c t k", k=RUN),
                     op=ALU.mult,
                 )
                 h_of[i].append(h)

@@ -1,3 +1,4 @@
+import math
 from contextlib import ExitStack
 
 import concourse.mybir as mybir
@@ -25,6 +26,15 @@ GROUPS = WIDTH // K_PASS
 HEADS_PER_GROUP = HEADS // GROUPS
 QUARTER = HEAD // PACK
 EPS = 1e-5
+
+DOWN = 2.0**-60
+SEED_BITS = 0x5FFFFFFF
+R_LOW = 2.0 * math.sqrt(2.0)
+R_HIGH = 16.0 / (3.0 * math.sqrt(3.0))
+RATIO = R_LOW**2 + R_LOW * R_HIGH + R_HIGH**2
+FIRST_B = 2.0 / (RATIO * (2.0 / 3.0 * math.sqrt(RATIO / 3.0) + R_LOW) - R_LOW**3)
+FIRST_A = RATIO * FIRST_B
+NEWTON = ((FIRST_A, FIRST_B), (1.5, 0.5), (1.5 * 2.0**-30, 0.5 * 2.0**-30))
 RUN = 4
 
 FLOPS = 2 * 2 * TOKENS * WIDTH * WIDTH
@@ -85,14 +95,14 @@ def tile_gatedmultiscaleretentionlayer_pa_kernel(
 
         load_ret(0)
         load_x(0)
+        load_ret(1)
         load_scales(wg_planes_raw, Wg_scales)
         load_words(wg_raw, Wg_words, 0)
         load_words(wg_raw, Wg_words, 1)
         load_x(1)
-        load_ret(1)
         load_ret(2)
-        load_x(2)
         load_ret(3)
+        load_x(2)
         load_scales(wo_planes, Wo_scales)
         load_words(wo_words, Wo_words, 0)
         load_words(wo_words, Wo_words, 1)
@@ -103,11 +113,9 @@ def tile_gatedmultiscaleretentionlayer_pa_kernel(
 
         ident = const.tile([P, P], F32)
         make_identity(nc, ident[:])
-        minus_half = const.tile([P, HEADS], F32)
-        nc.gpsimd.memset(minus_half[:], -0.5)
 
         warm = const.tile([P, 1], F32)
-        nc.scalar.activation(out=warm[:], in_=minus_half[:, 0:1], func=ACT.Silu)
+        nc.scalar.activation(out=warm[:], in_=ident[:, 0:1], func=ACT.Silu)
 
         bg_bf16 = const.tile([P, GROUPS, PACK], BF16)
         nc.gpsimd.dma_start(
@@ -131,6 +139,12 @@ def tile_gatedmultiscaleretentionlayer_pa_kernel(
                 )
                 nc.scalar.copy(out=bo_all[:, n], in_=spread[:])
 
+        waiting = []
+
+        def one_short():
+            if waiting:
+                waiting.pop(0)()
+
         wg_words = const.tile([P, GROUPS, WIDTH], U32, align_bytes=64)
         wg_planes = const.tile([P, WIDTH], U8, align_bytes=64)
 
@@ -140,42 +154,71 @@ def tile_gatedmultiscaleretentionlayer_pa_kernel(
                 out=wg_planes[:, columns].rearrange("p (t m) -> p t m", t=PACK),
                 in_=wg_planes_raw[:, columns].rearrange("p (m t) -> p t m", t=PACK),
             )
+            one_short()
             for g in range(GROUPS):
                 nc.vector.tensor_copy(
                     out=wg_words[:, g, columns].bitcast(I32).rearrange("p (t m) -> p t m", t=PACK),
                     in_=wg_raw[:, g, columns].bitcast(I32).rearrange("p (m t) -> p t m", t=PACK),
                 )
+                one_short()
 
-        affine_of, cat_of, ct_of = {}, {}, {}
+        stats_of, affine_of, cat_of, ct_of = {}, {}, {}, {}
         xt_of, xg_of, xq_of, zt_of, gate_of, h_of, hq_of, o_of = {}, {}, {}, {}, {}, {}, {}, {}
 
         def statistics(i):
-            stats = small.tile([P, HEADS // 2, 6], F32)
+            if i % 2 == 0:
+                stats_of[i] = small.tile([P, 2, HEADS // 2, 6], F32, name="stats")
+            stats = stats_of[i - i % 2]
             for pair in range(HEADS // 2):
                 nc.vector.bn_stats(
-                    out=stats[:, pair, :],
+                    out=stats[:, i % 2, pair, :],
                     in_=ret_sb[i][:, 2 * pair * HEAD : 2 * (pair + 1) * HEAD].rearrange(
                         "p (h c) -> p c h", h=2
                     ),
                 )
-            by_head = stats[:].rearrange("p k (e s) -> p (k e) s", e=2)
+                one_short()
+
+        def queue_affine(i):
+            by_head = stats_of[i][:].rearrange("p i k (e s) -> p (i k e) s", e=2)
             mean, m2 = by_head[:, :, 1], by_head[:, :, 2]
-            var = small.tile([P, HEADS], F32)
-            nc.gpsimd.tensor_scalar(
-                out=var[:], in0=m2, scalar1=1.0 / HEAD, scalar2=EPS, op0=ALU.mult, op1=ALU.add
-            )
-            minus_mean = small.tile([P, HEADS], F32)
-            nc.gpsimd.tensor_scalar(
-                out=minus_mean[:], in0=mean, scalar1=-1.0, scalar2=0.0, op0=ALU.mult, op1=ALU.add
-            )
-            rstd = small.tile([P, HEADS], F32)
-            nc.gpsimd.tensor_tensor(out=rstd[:], in0=var[:], in1=minus_half[:], op=ALU.pow)
-            shift = small.tile([P, HEADS], F32)
-            nc.gpsimd.tensor_tensor(out=shift[:], in0=minus_mean[:], in1=rstd[:], op=ALU.mult)
-            affine_of[i] = (rstd, shift)
+            columns = 2 * HEADS
+            w = small.tile([P, columns], F32)
+            waiting.append(lambda: nc.vector.tensor_scalar(
+                out=w[:], in0=m2, scalar1=DOWN / HEAD, scalar2=EPS * DOWN,
+                op0=ALU.mult, op1=ALU.add,
+            ))
+            bits = small.tile([P, columns], I32)
+            waiting.append(lambda: nc.vector.tensor_scalar(
+                out=bits[:], in0=w[:].bitcast(I32), scalar1=1, scalar2=SEED_BITS,
+                op0=ALU.logical_shift_right, op1=ALU.bitwise_xor,
+            ))
+
+            def newton(step, a, b, y):
+                square = small.tile([P, columns], F32, name="square%d" % step)
+                waiting.append(lambda: nc.vector.scalar_tensor_tensor(
+                    out=square[:], in0=y, scalar=-b, in1=y, op0=ALU.mult, op1=ALU.mult
+                ))
+                part = small.tile([P, columns], F32, name="part%d" % step)
+                waiting.append(lambda: nc.vector.tensor_tensor(
+                    out=part[:], in0=square[:], in1=w[:], op=ALU.mult
+                ))
+                better = small.tile([P, columns], F32, name="better%d" % step)
+                waiting.append(lambda: nc.vector.scalar_tensor_tensor(
+                    out=better[:], in0=part[:], scalar=a, in1=y, op0=ALU.add, op1=ALU.mult
+                ))
+                return better[:]
+
+            y = bits[:].bitcast(F32)
+            for step, (a, b) in enumerate(NEWTON):
+                y = newton(step, a, b, y)
+            shift = small.tile([P, columns], F32)
+            waiting.append(lambda: nc.vector.scalar_tensor_tensor(
+                out=shift[:], in0=mean, scalar=-1.0, in1=y, op0=ALU.mult, op1=ALU.mult
+            ))
+            affine_of[i], affine_of[i + 1] = (y, shift, 0), (y, shift, HEADS)
 
         def normalise(i):
-            rstd, shift = affine_of[i]
+            rstd, shift, first = affine_of[i]
             cat = work.tile([P, GROUPS, PACK, P], F32)
             for head in range(HEADS):
                 g, j = divmod(head, HEADS_PER_GROUP)
@@ -185,8 +228,8 @@ def tile_gatedmultiscaleretentionlayer_pa_kernel(
                         "p (c t) -> p t c", t=PACK
                     ),
                     func=ACT.Identity,
-                    scale=rstd[:, head : head + 1],
-                    bias=shift[:, head : head + 1],
+                    scale=rstd[:, first + head : first + head + 1],
+                    bias=shift[:, first + head : first + head + 1],
                 )
             cat_of[i] = cat
 
@@ -230,6 +273,7 @@ def tile_gatedmultiscaleretentionlayer_pa_kernel(
                 in_=xg_of[i][:],
             )
             xq_of[i] = (xq_words, xq_scales)
+            one_short()
 
         def gate_half(i, n):
             xq_words, xq_scales = xq_of[i]
@@ -276,6 +320,7 @@ def tile_gatedmultiscaleretentionlayer_pa_kernel(
                     op=ALU.mult,
                 )
                 h_of[i].append(h)
+                one_short()
 
         def quantise_h(i):
             hq_of[i] = []
@@ -288,6 +333,7 @@ def tile_gatedmultiscaleretentionlayer_pa_kernel(
                     in_=h_of[i][g][:].rearrange("p r t -> p (r t)"),
                 )
                 hq_of[i].append((hq_words, hq_scales))
+                one_short()
 
         def project(i):
             if i == TILES - 1:
@@ -313,15 +359,23 @@ def tile_gatedmultiscaleretentionlayer_pa_kernel(
                 nc.vector.tensor_tensor(
                     out=result[:], in0=o_of[i][n][:], in1=bo_all[:, n], op=ALU.add
                 )
+                one_short()
                 nc.sync.dma_start(out=out_rows[:, i, n * BANK : (n + 1) * BANK], in_=result[:])
 
         def each(step, i):
             if 0 <= i < TILES:
                 step(i)
 
-        statistics(0)
+        def statistics_and_affine(i):
+            statistics(i)
+            if i % 2 == 1:
+                queue_affine(i - 1)
+
+        statistics_and_affine(0)
         transpose_x(0)
         group_x(0)
+        statistics_and_affine(1)
+        one_short()
         sort_columns(0)
         quantise_x(0)
         sort_columns(1)
@@ -330,28 +384,30 @@ def tile_gatedmultiscaleretentionlayer_pa_kernel(
         gate_half(0, 1)
         silu_half(0, 0)
         group_x(1)
+        statistics_and_affine(2)
         normalise(0)
         silu_half(0, 1)
         transpose_cat(0)
-        statistics(1)
+        statistics_and_affine(3)
+        one_short()
         quantise_x(1)
+        one_short()
         transpose_x(2)
         group_x(2)
         normalise(1)
-        statistics(2)
-        statistics(3)
         for r in range(TILES + 1):
+            if r + 4 < TILES:
+                statistics_and_affine(r + 4)
             each(product, r)
             each(transpose_x, r + 3)
             each(group_x, r + 3)
             each(gate_matmul, r + 1)
             each(silu, r + 1)
-            each(normalise, r + 2)
-            each(project, r - 1)
-            each(transpose_cat, r + 1)
-            each(statistics, r + 4)
             each(quantise_h, r)
             each(quantise_x, r + 2)
+            each(project, r - 1)
+            each(transpose_cat, r + 1)
             if r == 0:
                 spread_bo()
             each(add_bo_and_store, r - 1)
+            each(normalise, r + 2)

@@ -35,6 +35,7 @@ RATIO = R_LOW**2 + R_LOW * R_HIGH + R_HIGH**2
 FIRST_B = 2.0 / (RATIO * (2.0 / 3.0 * math.sqrt(RATIO / 3.0) + R_LOW) - R_LOW**3)
 FIRST_A = RATIO * FIRST_B
 NEWTON = ((FIRST_A, FIRST_B), (1.5, 0.5), (1.5 * 2.0**-30, 0.5 * 2.0**-30))
+AFFINE_GROUPS = ((0, 1), (2, 3), (4, 5), (6, 7))
 RUN = 4
 
 FLOPS = 2 * 2 * TOKENS * WIDTH * WIDTH
@@ -64,6 +65,9 @@ def tile_gatedmultiscaleretentionlayer_pa_kernel(
         nc.vector.memset(wg_planes_raw[:].bitcast(I32), 0)
         wo_planes = const.tile([P, WIDTH], U8, align_bytes=64)
         nc.vector.memset(wo_planes[:].bitcast(I32), 0)
+
+        bo_row = const.tile([P, WIDTH], BF16)
+        nc.vector.memset(bo_row[:].bitcast(I32), 0)
 
         x_sb = [const.tile([P, WIDTH], BF16, name="x%d" % i) for i in range(TILES)]
         ret_sb = [const.tile([P, WIDTH], BF16, name="ret%d" % i) for i in range(TILES)]
@@ -95,6 +99,7 @@ def tile_gatedmultiscaleretentionlayer_pa_kernel(
 
         load_ret(0)
         load_x(0)
+        nc.sync.dma_start(out=bo_row[0:1, :], in_=bo.unsqueeze(0))
         load_ret(1)
         load_scales(wg_planes_raw, Wg_scales)
         load_words(wg_raw, Wg_words, 0)
@@ -103,13 +108,18 @@ def tile_gatedmultiscaleretentionlayer_pa_kernel(
         load_ret(2)
         load_ret(3)
         load_x(2)
+        load_ret(4)
+        load_x(3)
         load_scales(wo_planes, Wo_scales)
         load_words(wo_words, Wo_words, 0)
         load_words(wo_words, Wo_words, 1)
-        for i in range(3, TILES):
-            load_x(i)
-            if i + 1 < TILES:
-                load_ret(i + 1)
+        load_x(4)
+        load_ret(5)
+        load_x(5)
+        load_ret(6)
+        load_x(6)
+        load_ret(7)
+        load_x(7)
 
         ident = const.tile([P, P], F32)
         make_identity(nc, ident[:])
@@ -117,17 +127,12 @@ def tile_gatedmultiscaleretentionlayer_pa_kernel(
         warm = const.tile([P, 1], F32)
         nc.scalar.activation(out=warm[:], in_=ident[:, 0:1], func=ACT.Silu)
 
-        bg_bf16 = const.tile([P, GROUPS, PACK], BF16)
-        nc.gpsimd.dma_start(
-            out=bg_bf16[:], in_=bg.rearrange("(g p t) -> p g t", g=GROUPS, t=PACK)
-        )
-        bg_columns = const.tile([P, GROUPS, PACK], F32)
-        bo_row = const.tile([P, WIDTH], BF16)
-        nc.gpsimd.memset(bo_row[:].bitcast(I32), 0)
-        nc.gpsimd.dma_start(out=bo_row[0:1, :], in_=bo.unsqueeze(0))
         ones = const.tile([P, P], BF16)
         nc.gpsimd.memset(ones[:], 1.0)
-        nc.gpsimd.tensor_copy(out=bg_columns[:], in_=bg_bf16[:])
+        bg_columns = const.tile([P, GROUPS, PACK], BF16)
+        nc.gpsimd.dma_start(
+            out=bg_columns[:], in_=bg.rearrange("(g p t) -> p g t", g=GROUPS, t=PACK)
+        )
         bo_all = const.tile([P, GROUPS, BANK], F32)
 
         def spread_bo():
@@ -148,13 +153,16 @@ def tile_gatedmultiscaleretentionlayer_pa_kernel(
         wg_words = const.tile([P, GROUPS, WIDTH], U32, align_bytes=64)
         wg_planes = const.tile([P, WIDTH], U8, align_bytes=64)
 
-        def sort_columns(n):
+        def sort_planes(n):
             columns = slice(n * BANK, (n + 1) * BANK)
             nc.vector.tensor_copy(
                 out=wg_planes[:, columns].rearrange("p (t m) -> p t m", t=PACK),
                 in_=wg_planes_raw[:, columns].rearrange("p (m t) -> p t m", t=PACK),
             )
             one_short()
+
+        def sort_words(n):
+            columns = slice(n * BANK, (n + 1) * BANK)
             for g in range(GROUPS):
                 nc.vector.tensor_copy(
                     out=wg_words[:, g, columns].bitcast(I32).rearrange("p (t m) -> p t m", t=PACK),
@@ -165,23 +173,29 @@ def tile_gatedmultiscaleretentionlayer_pa_kernel(
         stats_of, affine_of, cat_of, ct_of = {}, {}, {}, {}
         xt_of, xg_of, xq_of, zt_of, gate_of, h_of, hq_of, o_of = {}, {}, {}, {}, {}, {}, {}, {}
 
+        def group_of(i):
+            return [group for group in AFFINE_GROUPS if i in group][0]
+
         def statistics(i):
-            if i % 2 == 0:
-                stats_of[i] = small.tile([P, 2, HEADS // 2, 6], F32, name="stats")
-            stats = stats_of[i - i % 2]
+            tiles = group_of(i)
+            if i == tiles[0]:
+                stats_of[i] = small.tile([P, len(tiles), HEADS // 2, 6], F32, name="stats")
+            stats = stats_of[tiles[0]]
             for pair in range(HEADS // 2):
                 nc.vector.bn_stats(
-                    out=stats[:, i % 2, pair, :],
+                    out=stats[:, i - tiles[0], pair, :],
                     in_=ret_sb[i][:, 2 * pair * HEAD : 2 * (pair + 1) * HEAD].rearrange(
                         "p (h c) -> p c h", h=2
                     ),
                 )
                 one_short()
+            if i == tiles[-1]:
+                queue_affine(tiles)
 
-        def queue_affine(i):
-            by_head = stats_of[i][:].rearrange("p i k (e s) -> p (i k e) s", e=2)
+        def queue_affine(tiles):
+            by_head = stats_of[tiles[0]][:].rearrange("p i k (e s) -> p (i k e) s", e=2)
             mean, m2 = by_head[:, :, 1], by_head[:, :, 2]
-            columns = 2 * HEADS
+            columns = len(tiles) * HEADS
             w = small.tile([P, columns], F32)
             waiting.append(lambda: nc.vector.tensor_scalar(
                 out=w[:], in0=m2, scalar1=DOWN / HEAD, scalar2=EPS * DOWN,
@@ -212,12 +226,19 @@ def tile_gatedmultiscaleretentionlayer_pa_kernel(
             for step, (a, b) in enumerate(NEWTON):
                 y = newton(step, a, b, y)
             shift = small.tile([P, columns], F32)
-            waiting.append(lambda: nc.vector.scalar_tensor_tensor(
-                out=shift[:], in0=mean, scalar=-1.0, in1=y, op0=ALU.mult, op1=ALU.mult
-            ))
-            affine_of[i], affine_of[i + 1] = (y, shift, 0), (y, shift, HEADS)
+
+            def last_short():
+                nc.vector.scalar_tensor_tensor(
+                    out=shift[:], in0=mean, scalar=-1.0, in1=y, op0=ALU.mult, op1=ALU.mult
+                )
+                for j, i in enumerate(tiles):
+                    affine_of[i] = (y, shift, j * HEADS)
+
+            waiting.append(last_short)
 
         def normalise(i):
+            while i not in affine_of:
+                waiting.pop(0)()
             rstd, shift, first = affine_of[i]
             cat = work.tile([P, GROUPS, PACK, P], F32)
             for head in range(HEADS):
@@ -233,20 +254,21 @@ def tile_gatedmultiscaleretentionlayer_pa_kernel(
                 )
             cat_of[i] = cat
 
-        def transpose_cat(i):
-            ct_of[i] = []
-            for g in range(GROUPS):
-                ct = psum_c.tile([P, PACK, P], F32, tag="ct")
-                for t in range(PACK):
-                    nc.tensor.transpose(
-                        out=ct[:, t, :], in_=cat_of[i][:, g, t, :], identity=ident[:]
-                    )
-                ct_of[i].append(ct)
+        def transpose_cat(i, g):
+            ct = psum_c.tile([P, PACK, P], F32, tag="ct")
+            for t in range(PACK):
+                nc.tensor.transpose(
+                    out=ct[:, t, :], in_=cat_of[i][:, g, t, :], identity=ident[:]
+                )
+            ct_of.setdefault(i, []).append(ct)
 
         def transpose_x(i):
             x_words = x_sb[i][:].bitcast(F32)
             pairs = K_PASS // 2
-            xt = psum_x.tile([P, GROUPS, 2, P], F32)
+            if i in ():
+                xt = psum_o.tile([P, GROUPS, 2, P], F32, tag="o")
+            else:
+                xt = psum_x.tile([P, GROUPS, 2, P], F32, tag="xt")
             for g in range(GROUPS):
                 for u in range(2):
                     nc.tensor.transpose(
@@ -297,7 +319,7 @@ def tile_gatedmultiscaleretentionlayer_pa_kernel(
                 gate_half(i, n)
 
         def silu_half(i, n):
-            gate = halves.tile([P, PACK, P], F32)
+            gate = halves.tile([P, PACK, P], F32, bufs=4)
             for t in range(PACK):
                 nc.scalar.activation(
                     out=gate[:, t, :], in_=zt_of[i][n][:, t, :], func=ACT.Silu,
@@ -309,31 +331,27 @@ def tile_gatedmultiscaleretentionlayer_pa_kernel(
             for n in range(GROUPS):
                 silu_half(i, n)
 
-        def product(i):
-            h_of[i] = []
-            for g in range(GROUPS):
-                h = halves.tile([P, P, PACK], BF16, align_bytes=64)
-                nc.vector.tensor_tensor(
-                    out=h[:].rearrange("p (c k) t -> p c t k", k=RUN),
-                    in0=ct_of[i][g][:].rearrange("p t (c k) -> p c t k", k=RUN),
-                    in1=gate_of[i][g][:].rearrange("p t (c k) -> p c t k", k=RUN),
-                    op=ALU.mult,
-                )
-                h_of[i].append(h)
-                one_short()
+        def product_half(i, g):
+            h = halves.tile([P, P, PACK], BF16, align_bytes=64)
+            nc.vector.tensor_tensor(
+                out=h[:].rearrange("p (c k) t -> p c t k", k=RUN),
+                in0=ct_of[i][g][:].rearrange("p t (c k) -> p c t k", k=RUN),
+                in1=gate_of[i][g][:].rearrange("p t (c k) -> p c t k", k=RUN),
+                op=ALU.mult,
+            )
+            h_of.setdefault(i, []).append(h)
+            one_short()
 
-        def quantise_h(i):
-            hq_of[i] = []
-            for g in range(GROUPS):
-                hq_words = halves.tile([P, P], U32, align_bytes=64)
-                hq_scales = halves.tile([P, P], U8, align_bytes=64)
-                nc.vector.quantize_mx(
-                    out=hq_words[:].bitcast(FP8X4),
-                    scales=hq_scales[:],
-                    in_=h_of[i][g][:].rearrange("p r t -> p (r t)"),
-                )
-                hq_of[i].append((hq_words, hq_scales))
-                one_short()
+        def quantise_h(i, g):
+            hq_words = halves.tile([P, P], U32, align_bytes=64)
+            hq_scales = halves.tile([P, P], U8, align_bytes=64)
+            nc.vector.quantize_mx(
+                out=hq_words[:].bitcast(FP8X4),
+                scales=hq_scales[:],
+                in_=h_of[i][g][:].rearrange("p r t -> p (r t)"),
+            )
+            hq_of.setdefault(i, []).append((hq_words, hq_scales))
+            one_short()
 
         def project(i):
             if i == TILES - 1:
@@ -353,61 +371,174 @@ def tile_gatedmultiscaleretentionlayer_pa_kernel(
                         stop=(g == GROUPS - 1),
                     )
 
-        def add_bo_and_store(i):
-            for n in range(GROUPS):
-                result = halves.tile([P, BANK], F32)
-                nc.vector.tensor_tensor(
-                    out=result[:], in0=o_of[i][n][:], in1=bo_all[:, n], op=ALU.add
-                )
-                one_short()
-                nc.sync.dma_start(out=out_rows[:, i, n * BANK : (n + 1) * BANK], in_=result[:])
+        def add_bo_and_store(i, n):
+            result = halves.tile([P, BANK], F32)
+            nc.vector.tensor_tensor(
+                out=result[:], in0=o_of[i][n][:], in1=bo_all[:, n], op=ALU.add
+            )
+            one_short()
+            nc.sync.dma_start(out=out_rows[:, i, n * BANK : (n + 1) * BANK], in_=result[:])
+
+        def scalar_add(i, n):
+            copied = halves.tile([P, BANK], F32)
+            nc.scalar.copy(out=copied[:], in_=o_of[i][n][:])
+            summed = halves.tile([P, BANK], F32)
+            nc.gpsimd.tensor_tensor(out=summed[:], in0=copied[:], in1=bo_all[:, n], op=ALU.add)
+            nc.sync.dma_start(out=out_rows[:, i, n * BANK : (n + 1) * BANK], in_=summed[:])
 
         def each(step, i):
             if 0 <= i < TILES:
                 step(i)
 
-        def statistics_and_affine(i):
-            statistics(i)
-            if i % 2 == 1:
-                queue_affine(i - 1)
-
-        statistics_and_affine(0)
+        statistics(0)
         transpose_x(0)
         group_x(0)
-        statistics_and_affine(1)
+        statistics(1)
         one_short()
-        sort_columns(0)
+        sort_planes(0)
+        sort_words(0)
         quantise_x(0)
-        sort_columns(1)
+        sort_planes(1)
+        sort_words(1)
         gate_half(0, 0)
         transpose_x(1)
         gate_half(0, 1)
         silu_half(0, 0)
         group_x(1)
-        statistics_and_affine(2)
+        statistics(2)
         normalise(0)
         silu_half(0, 1)
-        transpose_cat(0)
-        statistics_and_affine(3)
+        transpose_cat(0, 0)
+        transpose_cat(0, 1)
+        statistics(3)
         one_short()
         quantise_x(1)
         one_short()
         transpose_x(2)
         group_x(2)
         normalise(1)
-        for r in range(TILES + 1):
-            if r + 4 < TILES:
-                statistics_and_affine(r + 4)
-            each(product, r)
-            each(transpose_x, r + 3)
-            each(group_x, r + 3)
-            each(gate_matmul, r + 1)
-            each(silu, r + 1)
-            each(quantise_h, r)
-            each(quantise_x, r + 2)
-            each(project, r - 1)
-            each(transpose_cat, r + 1)
-            if r == 0:
-                spread_bo()
-            each(add_bo_and_store, r - 1)
-            each(normalise, r + 2)
+        spread_bo()
+        statistics(4)
+        product_half(0, 0)
+        product_half(0, 1)
+        transpose_x(3)
+        group_x(3)
+        gate_half(1, 0)
+        gate_half(1, 1)
+        silu_half(1, 0)
+        silu_half(1, 1)
+        quantise_h(0, 0)
+        quantise_h(0, 1)
+        quantise_x(2)
+        transpose_cat(1, 0)
+        transpose_cat(1, 1)
+        normalise(2)
+        statistics(5)
+        product_half(1, 0)
+        product_half(1, 1)
+        transpose_x(4)
+        group_x(4)
+        gate_half(2, 0)
+        gate_half(2, 1)
+        silu_half(2, 0)
+        silu_half(2, 1)
+        quantise_h(1, 0)
+        quantise_h(1, 1)
+        quantise_x(3)
+        project(0)
+        transpose_cat(2, 0)
+        transpose_cat(2, 1)
+        add_bo_and_store(0, 0)
+        add_bo_and_store(0, 1)
+        normalise(3)
+        statistics(6)
+        product_half(2, 0)
+        product_half(2, 1)
+        transpose_x(5)
+        group_x(5)
+        gate_half(3, 0)
+        gate_half(3, 1)
+        silu_half(3, 0)
+        silu_half(3, 1)
+        quantise_h(2, 0)
+        quantise_h(2, 1)
+        quantise_x(4)
+        project(1)
+        transpose_cat(3, 0)
+        transpose_cat(3, 1)
+        add_bo_and_store(1, 0)
+        add_bo_and_store(1, 1)
+        normalise(4)
+        statistics(7)
+        product_half(3, 0)
+        product_half(3, 1)
+        transpose_x(6)
+        group_x(6)
+        gate_half(4, 0)
+        gate_half(4, 1)
+        silu_half(4, 0)
+        silu_half(4, 1)
+        quantise_h(3, 0)
+        quantise_h(3, 1)
+        quantise_x(5)
+        project(2)
+        transpose_cat(4, 0)
+        transpose_cat(4, 1)
+        add_bo_and_store(2, 0)
+        add_bo_and_store(2, 1)
+        normalise(5)
+        product_half(4, 0)
+        product_half(4, 1)
+        transpose_x(7)
+        group_x(7)
+        gate_half(5, 0)
+        gate_half(5, 1)
+        silu_half(5, 0)
+        silu_half(5, 1)
+        quantise_h(4, 0)
+        quantise_h(4, 1)
+        quantise_x(6)
+        project(3)
+        transpose_cat(5, 0)
+        transpose_cat(5, 1)
+        add_bo_and_store(3, 0)
+        add_bo_and_store(3, 1)
+        normalise(6)
+        product_half(5, 0)
+        product_half(5, 1)
+        gate_half(6, 0)
+        gate_half(6, 1)
+        silu_half(6, 0)
+        silu_half(6, 1)
+        quantise_h(5, 0)
+        quantise_h(5, 1)
+        quantise_x(7)
+        project(4)
+        transpose_cat(6, 0)
+        transpose_cat(6, 1)
+        add_bo_and_store(4, 0)
+        add_bo_and_store(4, 1)
+        normalise(7)
+        product_half(6, 0)
+        product_half(6, 1)
+        gate_half(7, 0)
+        gate_half(7, 1)
+        silu_half(7, 0)
+        silu_half(7, 1)
+        quantise_h(6, 0)
+        quantise_h(6, 1)
+        project(5)
+        transpose_cat(7, 0)
+        transpose_cat(7, 1)
+        add_bo_and_store(5, 0)
+        add_bo_and_store(5, 1)
+        product_half(7, 0)
+        product_half(7, 1)
+        quantise_h(7, 0)
+        quantise_h(7, 1)
+        project(6)
+        add_bo_and_store(6, 0)
+        add_bo_and_store(6, 1)
+        project(7)
+        add_bo_and_store(7, 0)
+        add_bo_and_store(7, 1)

@@ -31,10 +31,29 @@ DOWN = 2.0**-60
 SEED_BITS = 0x5FFFFFFF
 R_LOW = 2.0 * math.sqrt(2.0)
 R_HIGH = 16.0 / (3.0 * math.sqrt(3.0))
-RATIO = R_LOW**2 + R_LOW * R_HIGH + R_HIGH**2
-FIRST_B = 2.0 / (RATIO * (2.0 / 3.0 * math.sqrt(RATIO / 3.0) + R_LOW) - R_LOW**3)
-FIRST_A = RATIO * FIRST_B
-NEWTON = ((FIRST_A, FIRST_B), (1.5, 0.5), (1.5 * 2.0**-30, 0.5 * 2.0**-30))
+UP = 2.0**-30
+MIDDLE, HALF_WIDTH = (R_HIGH**2 + R_LOW**2) / 2.0, (R_HIGH**2 - R_LOW**2) / 2.0
+NODES = [MIDDLE + HALF_WIDTH * math.cos(math.pi * (2 * k + 1) / 8.0) for k in range(4)]
+
+
+def divided(nodes):
+    if len(nodes) == 1:
+        return nodes[0] ** -0.5
+    return (divided(nodes[1:]) - divided(nodes[:-1])) / (nodes[-1] - nodes[0])
+
+
+def cubic():
+    total = [0.0] * 4
+    basis = [1.0]
+    for k in range(4):
+        factor = divided(NODES[: k + 1])
+        total = [t + factor * (basis[j] if j < len(basis) else 0.0) for j, t in enumerate(total)]
+        shifted = [0.0] + basis
+        basis = [s - NODES[k] * (basis[j] if j < len(basis) else 0.0) for j, s in enumerate(shifted)]
+    return total[3], [t / total[3] for t in total[:3]]
+
+
+LEAD, CUBIC = cubic()
 AFFINE_GROUPS = ((0, 1), (2, 3), (4, 5), (6, 7))
 RUN = 4
 
@@ -53,7 +72,7 @@ def tile_gatedmultiscaleretentionlayer_pa_kernel(
     with ExitStack() as stack:
         const = stack.enter_context(tc.tile_pool(name="const", bufs=1))
         small = stack.enter_context(tc.tile_pool(name="small", bufs=4))
-        work = stack.enter_context(tc.tile_pool(name="work", bufs=3))
+        work = stack.enter_context(tc.tile_pool(name="work", bufs=4))
         halves = stack.enter_context(tc.tile_pool(name="halves", bufs=4))
         psum_x = stack.enter_context(tc.psum_pool(name="psum_x", bufs=1))
         psum_z = stack.enter_context(tc.psum_pool(name="psum_z", bufs=2))
@@ -106,8 +125,8 @@ def tile_gatedmultiscaleretentionlayer_pa_kernel(
         load_words(wg_raw, Wg_words, 1)
         load_x(1)
         load_ret(2)
-        load_ret(3)
         load_x(2)
+        load_ret(3)
         load_ret(4)
         load_x(3)
         load_scales(wo_planes, Wo_scales)
@@ -207,24 +226,23 @@ def tile_gatedmultiscaleretentionlayer_pa_kernel(
                 op0=ALU.logical_shift_right, op1=ALU.bitwise_xor,
             ))
 
-            def newton(step, a, b, y):
-                square = small.tile([P, columns], F32, name="square%d" % step)
-                waiting.append(lambda: nc.vector.scalar_tensor_tensor(
-                    out=square[:], in0=y, scalar=-b, in1=y, op0=ALU.mult, op1=ALU.mult
-                ))
-                part = small.tile([P, columns], F32, name="part%d" % step)
-                waiting.append(lambda: nc.vector.tensor_tensor(
-                    out=part[:], in0=square[:], in1=w[:], op=ALU.mult
-                ))
-                better = small.tile([P, columns], F32, name="better%d" % step)
-                waiting.append(lambda: nc.vector.scalar_tensor_tensor(
-                    out=better[:], in0=part[:], scalar=a, in1=y, op0=ALU.add, op1=ALU.mult
-                ))
-                return better[:]
+            def later(name, **call):
+                made = small.tile([P, columns], F32, name=name)
+                if "scalar" in call:
+                    waiting.append(lambda: nc.vector.scalar_tensor_tensor(out=made[:], **call))
+                else:
+                    waiting.append(lambda: nc.vector.tensor_tensor(out=made[:], **call))
+                return made[:]
 
             y = bits[:].bitcast(F32)
-            for step, (a, b) in enumerate(NEWTON):
-                y = newton(step, a, b, y)
+            square = later("square", in0=y, in1=y, op=ALU.mult)
+            a = later("a", in0=square, in1=w[:], op=ALU.mult)
+            sum2 = later("sum2", in0=a, scalar=CUBIC[2], in1=a, op0=ALU.add, op1=ALU.mult)
+            sum1 = later("sum1", in0=sum2, scalar=CUBIC[1], in1=a, op0=ALU.add, op1=ALU.mult)
+            y = later("close", in0=sum1, scalar=CUBIC[0], in1=y, op0=ALU.add, op1=ALU.mult)
+            square = later("square1", in0=y, scalar=-0.5 * LEAD**3 * UP, in1=y, op0=ALU.mult, op1=ALU.mult)
+            a = later("a1", in0=square, in1=w[:], op=ALU.mult)
+            y = later("rstd", in0=a, scalar=1.5 * LEAD * UP, in1=y, op0=ALU.add, op1=ALU.mult)
             shift = small.tile([P, columns], F32)
 
             def last_short():
@@ -372,7 +390,7 @@ def tile_gatedmultiscaleretentionlayer_pa_kernel(
                     )
 
         def add_bo_and_store(i, n):
-            result = halves.tile([P, BANK], F32)
+            result = halves.tile([P, BANK], F32, bufs=8)
             nc.vector.tensor_tensor(
                 out=result[:], in0=o_of[i][n][:], in1=bo_all[:, n], op=ALU.add
             )
@@ -467,7 +485,7 @@ def tile_gatedmultiscaleretentionlayer_pa_kernel(
         transpose_cat(3, 0)
         transpose_cat(3, 1)
         add_bo_and_store(1, 0)
-        add_bo_and_store(1, 1)
+        scalar_add(1, 1)
         normalise(4)
         statistics(7)
         product_half(3, 0)
@@ -485,7 +503,7 @@ def tile_gatedmultiscaleretentionlayer_pa_kernel(
         transpose_cat(4, 0)
         transpose_cat(4, 1)
         add_bo_and_store(2, 0)
-        add_bo_and_store(2, 1)
+        scalar_add(2, 1)
         normalise(5)
         product_half(4, 0)
         product_half(4, 1)
@@ -502,7 +520,7 @@ def tile_gatedmultiscaleretentionlayer_pa_kernel(
         transpose_cat(5, 0)
         transpose_cat(5, 1)
         add_bo_and_store(3, 0)
-        add_bo_and_store(3, 1)
+        scalar_add(3, 1)
         normalise(6)
         product_half(5, 0)
         product_half(5, 1)

@@ -144,10 +144,10 @@ def tile_gatedmultiscaleretentionlayer_pa_kernel(
         make_identity(nc, ident[:])
 
         warm = const.tile([P, 1], F32)
-        nc.scalar.activation(out=warm[:], in_=ident[:, 0:1], func=ACT.Silu)
-
         ones = const.tile([P, P], BF16)
         nc.gpsimd.memset(ones[:], 1.0)
+        nc.scalar.activation(out=warm[:], in_=ones[:, 0:1], func=ACT.Abs_reciprocal_sqrt)
+
         bg_columns = const.tile([P, GROUPS, PACK], BF16)
         nc.gpsimd.dma_start(
             out=bg_columns[:], in_=bg.rearrange("(g p t) -> p g t", g=GROUPS, t=PACK)
@@ -215,34 +215,58 @@ def tile_gatedmultiscaleretentionlayer_pa_kernel(
             by_head = stats_of[tiles[0]][:].rearrange("p i k (e s) -> p (i k e) s", e=2)
             mean, m2 = by_head[:, :, 1], by_head[:, :, 2]
             columns = len(tiles) * HEADS
-            w = small.tile([P, columns], F32)
-            waiting.append(lambda: nc.vector.tensor_scalar(
-                out=w[:], in0=m2, scalar1=DOWN / HEAD, scalar2=EPS * DOWN,
-                op0=ALU.mult, op1=ALU.add,
-            ))
-            bits = small.tile([P, columns], I32)
-            waiting.append(lambda: nc.vector.tensor_scalar(
-                out=bits[:], in0=w[:].bitcast(I32), scalar1=1, scalar2=SEED_BITS,
-                op0=ALU.logical_shift_right, op1=ALU.bitwise_xor,
-            ))
+            if tiles[0] == 0:
+                w0 = small.tile([P, columns], F32)
+                nc.vector.tensor_scalar(
+                    out=w0[:], in0=m2, scalar1=1.0 / HEAD, scalar2=EPS, op0=ALU.mult, op1=ALU.add
+                )
+                rough = small.tile([P, columns], F32)
+                nc.scalar.activation(out=rough[:], in_=w0[:], func=ACT.Abs_reciprocal_sqrt)
+                nc.scalar.activation(out=warm[:], in_=ones[:, 0:1], func=ACT.Silu)
+                square0 = small.tile([P, columns], F32, name="square9")
+                waiting.append(lambda: nc.vector.scalar_tensor_tensor(
+                    out=square0[:], in0=rough[:], scalar=-0.5, in1=rough[:],
+                    op0=ALU.mult, op1=ALU.mult,
+                ))
+                part0 = small.tile([P, columns], F32, name="part9")
+                waiting.append(lambda: nc.vector.tensor_tensor(
+                    out=part0[:], in0=square0[:], in1=w0[:], op=ALU.mult
+                ))
+                better0 = small.tile([P, columns], F32, name="better9")
+                waiting.append(lambda: nc.vector.scalar_tensor_tensor(
+                    out=better0[:], in0=part0[:], scalar=1.5, in1=rough[:],
+                    op0=ALU.add, op1=ALU.mult,
+                ))
+                y = better0[:]
+            else:
+                w = small.tile([P, columns], F32)
+                waiting.append(lambda: nc.vector.tensor_scalar(
+                    out=w[:], in0=m2, scalar1=DOWN / HEAD, scalar2=EPS * DOWN,
+                    op0=ALU.mult, op1=ALU.add,
+                ))
+                bits = small.tile([P, columns], I32)
+                waiting.append(lambda: nc.vector.tensor_scalar(
+                    out=bits[:], in0=w[:].bitcast(I32), scalar1=1, scalar2=SEED_BITS,
+                    op0=ALU.logical_shift_right, op1=ALU.bitwise_xor,
+                ))
 
-            def later(name, **call):
-                made = small.tile([P, columns], F32, name=name)
-                if "scalar" in call:
-                    waiting.append(lambda: nc.vector.scalar_tensor_tensor(out=made[:], **call))
-                else:
-                    waiting.append(lambda: nc.vector.tensor_tensor(out=made[:], **call))
-                return made[:]
+                def later(name, **call):
+                    made = small.tile([P, columns], F32, name=name)
+                    if "scalar" in call:
+                        waiting.append(lambda: nc.vector.scalar_tensor_tensor(out=made[:], **call))
+                    else:
+                        waiting.append(lambda: nc.vector.tensor_tensor(out=made[:], **call))
+                    return made[:]
 
-            y = bits[:].bitcast(F32)
-            square = later("square", in0=y, in1=y, op=ALU.mult)
-            a = later("a", in0=square, in1=w[:], op=ALU.mult)
-            sum2 = later("sum2", in0=a, scalar=CUBIC[2], in1=a, op0=ALU.add, op1=ALU.mult)
-            sum1 = later("sum1", in0=sum2, scalar=CUBIC[1], in1=a, op0=ALU.add, op1=ALU.mult)
-            y = later("close", in0=sum1, scalar=CUBIC[0], in1=y, op0=ALU.add, op1=ALU.mult)
-            square = later("square1", in0=y, scalar=-0.5 * LEAD**3 * UP, in1=y, op0=ALU.mult, op1=ALU.mult)
-            a = later("a1", in0=square, in1=w[:], op=ALU.mult)
-            y = later("rstd", in0=a, scalar=1.5 * LEAD * UP, in1=y, op0=ALU.add, op1=ALU.mult)
+                y = bits[:].bitcast(F32)
+                square = later("square", in0=y, in1=y, op=ALU.mult)
+                a = later("a", in0=square, in1=w[:], op=ALU.mult)
+                sum2 = later("sum2", in0=a, scalar=CUBIC[2], in1=a, op0=ALU.add, op1=ALU.mult)
+                sum1 = later("sum1", in0=sum2, scalar=CUBIC[1], in1=a, op0=ALU.add, op1=ALU.mult)
+                y = later("close", in0=sum1, scalar=CUBIC[0], in1=y, op0=ALU.add, op1=ALU.mult)
+                square = later("square1", in0=y, scalar=-0.5 * LEAD**3 * UP, in1=y, op0=ALU.mult, op1=ALU.mult)
+                a = later("a1", in0=square, in1=w[:], op=ALU.mult)
+                y = later("rstd", in0=a, scalar=1.5 * LEAD * UP, in1=y, op0=ALU.add, op1=ALU.mult)
             shift = small.tile([P, columns], F32)
 
             def last_short():
@@ -439,6 +463,7 @@ def tile_gatedmultiscaleretentionlayer_pa_kernel(
         statistics(4)
         product_half(0, 0)
         product_half(0, 1)
+        quantise_x(2)
         transpose_x(3)
         group_x(3)
         gate_half(1, 0)
@@ -447,13 +472,13 @@ def tile_gatedmultiscaleretentionlayer_pa_kernel(
         silu_half(1, 1)
         quantise_h(0, 0)
         quantise_h(0, 1)
-        quantise_x(2)
         transpose_cat(1, 0)
         transpose_cat(1, 1)
         normalise(2)
         statistics(5)
         product_half(1, 0)
         product_half(1, 1)
+        quantise_x(3)
         transpose_x(4)
         group_x(4)
         gate_half(2, 0)
@@ -462,7 +487,6 @@ def tile_gatedmultiscaleretentionlayer_pa_kernel(
         silu_half(2, 1)
         quantise_h(1, 0)
         quantise_h(1, 1)
-        quantise_x(3)
         project(0)
         transpose_cat(2, 0)
         transpose_cat(2, 1)
@@ -472,6 +496,7 @@ def tile_gatedmultiscaleretentionlayer_pa_kernel(
         statistics(6)
         product_half(2, 0)
         product_half(2, 1)
+        quantise_x(4)
         transpose_x(5)
         group_x(5)
         gate_half(3, 0)
@@ -480,7 +505,6 @@ def tile_gatedmultiscaleretentionlayer_pa_kernel(
         silu_half(3, 1)
         quantise_h(2, 0)
         quantise_h(2, 1)
-        quantise_x(4)
         project(1)
         transpose_cat(3, 0)
         transpose_cat(3, 1)
@@ -490,6 +514,7 @@ def tile_gatedmultiscaleretentionlayer_pa_kernel(
         statistics(7)
         product_half(3, 0)
         product_half(3, 1)
+        quantise_x(5)
         transpose_x(6)
         group_x(6)
         gate_half(4, 0)
@@ -498,7 +523,6 @@ def tile_gatedmultiscaleretentionlayer_pa_kernel(
         silu_half(4, 1)
         quantise_h(3, 0)
         quantise_h(3, 1)
-        quantise_x(5)
         project(2)
         transpose_cat(4, 0)
         transpose_cat(4, 1)
@@ -507,6 +531,7 @@ def tile_gatedmultiscaleretentionlayer_pa_kernel(
         normalise(5)
         product_half(4, 0)
         product_half(4, 1)
+        quantise_x(6)
         transpose_x(7)
         group_x(7)
         gate_half(5, 0)
@@ -515,7 +540,6 @@ def tile_gatedmultiscaleretentionlayer_pa_kernel(
         silu_half(5, 1)
         quantise_h(4, 0)
         quantise_h(4, 1)
-        quantise_x(6)
         project(3)
         transpose_cat(5, 0)
         transpose_cat(5, 1)
@@ -524,18 +548,18 @@ def tile_gatedmultiscaleretentionlayer_pa_kernel(
         normalise(6)
         product_half(5, 0)
         product_half(5, 1)
+        quantise_x(7)
         gate_half(6, 0)
         gate_half(6, 1)
         silu_half(6, 0)
         silu_half(6, 1)
         quantise_h(5, 0)
         quantise_h(5, 1)
-        quantise_x(7)
         project(4)
         transpose_cat(6, 0)
         transpose_cat(6, 1)
         add_bo_and_store(4, 0)
-        add_bo_and_store(4, 1)
+        scalar_add(4, 1)
         normalise(7)
         product_half(6, 0)
         product_half(6, 1)
@@ -549,7 +573,7 @@ def tile_gatedmultiscaleretentionlayer_pa_kernel(
         transpose_cat(7, 0)
         transpose_cat(7, 1)
         add_bo_and_store(5, 0)
-        add_bo_and_store(5, 1)
+        scalar_add(5, 1)
         product_half(7, 0)
         product_half(7, 1)
         quantise_h(7, 0)

@@ -154,6 +154,14 @@ def tile_gatedmultiscaleretentionlayer_pa_kernel(
         )
         bo_all = const.tile([P, GROUPS, BANK], F32)
 
+        spread_of = []
+
+        def warm_tensor():
+            dummy = psum_o.tile([P, BANK], F32, tag="o")
+            nc.tensor.matmul(
+                out=dummy[:], lhsT=ones[:], rhs=bo_row[:, 0:BANK], start=True, stop=True
+            )
+
         def spread_bo():
             for n in range(GROUPS):
                 spread = psum_o.tile([P, BANK], F32, tag="o")
@@ -161,7 +169,11 @@ def tile_gatedmultiscaleretentionlayer_pa_kernel(
                     out=spread[:], lhsT=ones[:], rhs=bo_row[:, n * BANK : (n + 1) * BANK],
                     start=True, stop=True,
                 )
-                nc.scalar.copy(out=bo_all[:, n], in_=spread[:])
+                spread_of.append(spread)
+
+        def keep_bo():
+            for n in range(GROUPS):
+                nc.scalar.copy(out=bo_all[:, n], in_=spread_of[n][:])
 
         waiting = []
 
@@ -436,7 +448,6 @@ def tile_gatedmultiscaleretentionlayer_pa_kernel(
         transpose_x(0)
         group_x(0)
         statistics(1)
-        one_short()
         sort_planes(0)
         sort_words(0)
         quantise_x(0)
@@ -445,6 +456,7 @@ def tile_gatedmultiscaleretentionlayer_pa_kernel(
         gate_half(0, 0)
         transpose_x(1)
         gate_half(0, 1)
+        warm_tensor()
         silu_half(0, 0)
         group_x(1)
         statistics(2)
@@ -470,6 +482,7 @@ def tile_gatedmultiscaleretentionlayer_pa_kernel(
         gate_half(1, 1)
         silu_half(1, 0)
         silu_half(1, 1)
+        keep_bo()
         quantise_h(0, 0)
         quantise_h(0, 1)
         transpose_cat(1, 0)
@@ -559,7 +572,7 @@ def tile_gatedmultiscaleretentionlayer_pa_kernel(
         transpose_cat(6, 0)
         transpose_cat(6, 1)
         add_bo_and_store(4, 0)
-        scalar_add(4, 1)
+        add_bo_and_store(4, 1)
         normalise(7)
         product_half(6, 0)
         product_half(6, 1)
@@ -573,7 +586,7 @@ def tile_gatedmultiscaleretentionlayer_pa_kernel(
         transpose_cat(7, 0)
         transpose_cat(7, 1)
         add_bo_and_store(5, 0)
-        scalar_add(5, 1)
+        add_bo_and_store(5, 1)
         product_half(7, 0)
         product_half(7, 1)
         quantise_h(7, 0)

@@ -158,9 +158,10 @@ def tile_gatedmultiscaleretentionlayer_pa_kernel(
 
         def warm_tensor():
             dummy = psum_o.tile([P, BANK], F32, tag="o")
-            nc.tensor.matmul(
-                out=dummy[:], lhsT=ones[:], rhs=bo_row[:, 0:BANK], start=True, stop=True
-            )
+            for repeat in range(1):
+                nc.tensor.matmul(
+                    out=dummy[:], lhsT=ones[:], rhs=bo_row[:, 0:BANK], start=True, stop=True
+                )
 
         def spread_bo():
             for n in range(GROUPS):
@@ -457,10 +458,10 @@ def tile_gatedmultiscaleretentionlayer_pa_kernel(
         transpose_x(1)
         gate_half(0, 1)
         warm_tensor()
+        normalise(0)
         silu_half(0, 0)
         group_x(1)
         statistics(2)
-        normalise(0)
         silu_half(0, 1)
         transpose_cat(0, 0)
         transpose_cat(0, 1)
@@ -506,7 +507,6 @@ def tile_gatedmultiscaleretentionlayer_pa_kernel(
         add_bo_and_store(0, 0)
         add_bo_and_store(0, 1)
         normalise(3)
-        statistics(6)
         product_half(2, 0)
         product_half(2, 1)
         quantise_x(4)
@@ -521,9 +521,10 @@ def tile_gatedmultiscaleretentionlayer_pa_kernel(
         project(1)
         transpose_cat(3, 0)
         transpose_cat(3, 1)
-        add_bo_and_store(1, 0)
+        scalar_add(1, 0)
         scalar_add(1, 1)
         normalise(4)
+        statistics(6)
         statistics(7)
         product_half(3, 0)
         product_half(3, 1)

import math
from contextlib import ExitStack

import concourse.mybir as mybir
from concourse.masks import make_identity

F32 = mybir.dt.float32
BF16 = mybir.dt.bfloat16
I32 = mybir.dt.int32
U32 = mybir.dt.uint32
U8 = mybir.dt.uint8
FP8X4 = mybir.dt.float8_e4m3fn_x4
ALU = mybir.AluOpType
ACT = mybir.ActivationFunctionType

P = 128
PACK = 4
K_PASS = P * PACK
BANK = 512
TOKENS = 32 * 32
WIDTH = 1024
HEADS = 8
HEAD = WIDTH // HEADS
TILES = TOKENS // P
GROUPS = WIDTH // K_PASS
HEADS_PER_GROUP = HEADS // GROUPS
QUARTER = HEAD // PACK
EPS = 1e-5

DOWN = 2.0**-60
SEED_BITS = 0x5FFFFFFF
R_LOW = 2.0 * math.sqrt(2.0)
R_HIGH = 16.0 / (3.0 * math.sqrt(3.0))
UP = 2.0**-30
MIDDLE, HALF_WIDTH = (R_HIGH**2 + R_LOW**2) / 2.0, (R_HIGH**2 - R_LOW**2) / 2.0
NODES = [MIDDLE + HALF_WIDTH * math.cos(math.pi * (2 * k + 1) / 8.0) for k in range(4)]


def divided(nodes):
    if len(nodes) == 1:
        return nodes[0] ** -0.5
    return (divided(nodes[1:]) - divided(nodes[:-1])) / (nodes[-1] - nodes[0])


def cubic():
    total = [0.0] * 4
    basis = [1.0]
    for k in range(4):
        factor = divided(NODES[: k + 1])
        total = [t + factor * (basis[j] if j < len(basis) else 0.0) for j, t in enumerate(total)]
        shifted = [0.0] + basis
        basis = [s - NODES[k] * (basis[j] if j < len(basis) else 0.0) for j, s in enumerate(shifted)]
    return total[3], [t / total[3] for t in total[:3]]


LEAD, CUBIC = cubic()
AFFINE_GROUPS = ((0, 1), (2, 3), (4, 5), (6, 7))
RUN = 4

FLOPS = 2 * 2 * TOKENS * WIDTH * WIDTH


def tile_gatedmultiscaleretentionlayer_pa_kernel(
    tc, x, ret_cat, Wg_words, Wg_scales, bg, Wo_words, Wo_scales, bo, out
):
    nc = tc.nc

    x_rows = x.flatten_outer_dims().rearrange("(p i) d -> p i d", i=TILES)
    ret_rows = ret_cat.flatten_outer_dims().rearrange("(p i) d -> p i d", i=TILES)
    out_rows = out.flatten_outer_dims().rearrange("(p i) d -> p i d", i=TILES)

    with ExitStack() as stack:
        const = stack.enter_context(tc.tile_pool(name="const", bufs=1))
        small = stack.enter_context(tc.tile_pool(name="small", bufs=4))
        work = stack.enter_context(tc.tile_pool(name="work", bufs=4))
        halves = stack.enter_context(tc.tile_pool(name="halves", bufs=4))
        psum_x = stack.enter_context(tc.psum_pool(name="psum_x", bufs=1))
        psum_z = stack.enter_context(tc.psum_pool(name="psum_z", bufs=2))
        psum_c = stack.enter_context(tc.psum_pool(name="psum_c", bufs=3))
        psum_o = stack.enter_context(tc.psum_pool(name="psum_o", bufs=2))
        stack.enter_context(tc.manual_schedule())

        wg_planes_raw = const.tile([P, WIDTH], U8, align_bytes=64)
        nc.vector.memset(wg_planes_raw[:].bitcast(I32), 0)
        wo_planes = const.tile([P, WIDTH], U8, align_bytes=64)
        nc.vector.memset(wo_planes[:].bitcast(I32), 0)

        bo_row = const.tile([P, WIDTH], BF16)
        nc.vector.memset(bo_row[:].bitcast(I32), 0)

        x_sb = [const.tile([P, WIDTH], BF16, name="x%d" % i) for i in range(TILES)]
        ret_sb = [const.tile([P, WIDTH], BF16, name="ret%d" % i) for i in range(TILES)]
        wg_raw = const.tile([P, GROUPS, WIDTH], U32, align_bytes=64)
        wo_words = const.tile([P, GROUPS, WIDTH], U32, align_bytes=64)

        def load_x(i):
            nc.sync.dma_start(out=x_sb[i][:], in_=x_rows[:, i, :])

        def load_ret(i):
            nc.sync.dma_start(out=ret_sb[i][:], in_=ret_rows[:, i, :])

        def load_scales(planes, scales):
            for quadrant in range(4):
                top = 32 * quadrant
                nc.sync.dma_start(
                    out=planes[top : top + PACK * GROUPS, :].bitcast(I32),
                    in_=scales[:, 4 * quadrant : 4 * quadrant + 4, :].bitcast(I32),
                )

        def load_words(words_sb, words, n):
            for g in range(GROUPS):
                nc.sync.dma_start(
                    out=words_sb[:, g, n * BANK : (n + 1) * BANK].bitcast(I32),
                    in_=words[g, :, n * BANK : (n + 1) * BANK, :]
                    .rearrange("p n t -> p (n t)")
                    .bitcast(I32),
                )

        load_ret(0)
        load_x(0)
        nc.sync.dma_start(out=bo_row[0:1, :], in_=bo.unsqueeze(0))
        load_ret(1)
        load_scales(wg_planes_raw, Wg_scales)
        load_words(wg_raw, Wg_words, 0)
        load_words(wg_raw, Wg_words, 1)
        load_x(1)
        load_ret(2)
        load_x(2)
        load_ret(3)
        load_ret(4)
        load_x(3)
        load_scales(wo_planes, Wo_scales)
        load_words(wo_words, Wo_words, 0)
        load_words(wo_words, Wo_words, 1)
        load_x(4)
        load_ret(5)
        load_x(5)
        load_ret(6)
        load_x(6)
        load_ret(7)
        load_x(7)

        ident = const.tile([P, P], F32)
        make_identity(nc, ident[:])

        warm = const.tile([P, 1], F32)
        ones = const.tile([P, P], BF16)
        nc.gpsimd.memset(ones[:], 1.0)
        nc.scalar.activation(out=warm[:], in_=ones[:, 0:1], func=ACT.Abs_reciprocal_sqrt)

        bg_columns = const.tile([P, GROUPS, PACK], BF16)
        nc.gpsimd.dma_start(
            out=bg_columns[:], in_=bg.rearrange("(g p t) -> p g t", g=GROUPS, t=PACK)
        )
        bo_all = const.tile([P, GROUPS, BANK], F32)

        spread_of = []

        def warm_tensor():
            dummy = psum_o.tile([P, BANK], F32, tag="o")
            for repeat in range(1):
                nc.tensor.matmul(
                    out=dummy[:], lhsT=ones[:], rhs=bo_row[:, 0:BANK], start=True, stop=True
                )

        def spread_bo():
            for n in range(GROUPS):
                spread = psum_o.tile([P, BANK], F32, tag="o")
                nc.tensor.matmul(
                    out=spread[:], lhsT=ones[:], rhs=bo_row[:, n * BANK : (n + 1) * BANK],
                    start=True, stop=True,
                )
                spread_of.append(spread)

        def keep_bo():
            for n in range(GROUPS):
                nc.scalar.copy(out=bo_all[:, n], in_=spread_of[n][:])

        waiting = []

        def one_short():
            if waiting:
                waiting.pop(0)()

        wg_words = const.tile([P, GROUPS, WIDTH], U32, align_bytes=64)
        wg_planes = const.tile([P, WIDTH], U8, align_bytes=64)

        def sort_planes(n):
            columns = slice(n * BANK, (n + 1) * BANK)
            nc.vector.tensor_copy(
                out=wg_planes[:, columns].rearrange("p (t m) -> p t m", t=PACK),
                in_=wg_planes_raw[:, columns].rearrange("p (m t) -> p t m", t=PACK),
            )
            one_short()

        def sort_words(n):
            columns = slice(n * BANK, (n + 1) * BANK)
            for g in range(GROUPS):
                nc.vector.tensor_copy(
                    out=wg_words[:, g, columns].bitcast(I32).rearrange("p (t m) -> p t m", t=PACK),
                    in_=wg_raw[:, g, columns].bitcast(I32).rearrange("p (m t) -> p t m", t=PACK),
                )
                one_short()

        stats_of, affine_of, cat_of, ct_of = {}, {}, {}, {}
        xt_of, xg_of, xq_of, zt_of, gate_of, h_of, hq_of, o_of = {}, {}, {}, {}, {}, {}, {}, {}

        def group_of(i):
            return [group for group in AFFINE_GROUPS if i in group][0]

        def statistics(i):
            tiles = group_of(i)
            if i == tiles[0]:
                stats_of[i] = small.tile([P, len(tiles), HEADS // 2, 6], F32, name="stats")
            stats = stats_of[tiles[0]]
            for pair in range(HEADS // 2):
                nc.vector.bn_stats(
                    out=stats[:, i - tiles[0], pair, :],
                    in_=ret_sb[i][:, 2 * pair * HEAD : 2 * (pair + 1) * HEAD].rearrange(
                        "p (h c) -> p c h", h=2
                    ),
                )
                one_short()
            if i == tiles[-1]:
                queue_affine(tiles)

        def queue_affine(tiles):
            by_head = stats_of[tiles[0]][:].rearrange("p i k (e s) -> p (i k e) s", e=2)
            mean, m2 = by_head[:, :, 1], by_head[:, :, 2]
            columns = len(tiles) * HEADS
            if tiles[0] == 0:
                w0 = small.tile([P, columns], F32)
                nc.vector.tensor_scalar(
                    out=w0[:], in0=m2, scalar1=1.0 / HEAD, scalar2=EPS, op0=ALU.mult, op1=ALU.add
                )
                rough = small.tile([P, columns], F32)
                nc.scalar.activation(out=rough[:], in_=w0[:], func=ACT.Abs_reciprocal_sqrt)
                nc.scalar.activation(out=warm[:], in_=ones[:, 0:1], func=ACT.Silu)
                square0 = small.tile([P, columns], F32, name="square9")
                waiting.append(lambda: nc.vector.scalar_tensor_tensor(
                    out=square0[:], in0=rough[:], scalar=-0.5, in1=rough[:],
                    op0=ALU.mult, op1=ALU.mult,
                ))
                part0 = small.tile([P, columns], F32, name="part9")
                waiting.append(lambda: nc.vector.tensor_tensor(
                    out=part0[:], in0=square0[:], in1=w0[:], op=ALU.mult
                ))
                better0 = small.tile([P, columns], F32, name="better9")
                waiting.append(lambda: nc.vector.scalar_tensor_tensor(
                    out=better0[:], in0=part0[:], scalar=1.5, in1=rough[:],
                    op0=ALU.add, op1=ALU.mult,
                ))
                y = better0[:]
            else:
                w = small.tile([P, columns], F32)
                waiting.append(lambda: nc.vector.tensor_scalar(
                    out=w[:], in0=m2, scalar1=DOWN / HEAD, scalar2=EPS * DOWN,
                    op0=ALU.mult, op1=ALU.add,
                ))
                bits = small.tile([P, columns], I32)
                waiting.append(lambda: nc.vector.tensor_scalar(
                    out=bits[:], in0=w[:].bitcast(I32), scalar1=1, scalar2=SEED_BITS,
                    op0=ALU.logical_shift_right, op1=ALU.bitwise_xor,
                ))

                def later(name, **call):
                    made = small.tile([P, columns], F32, name=name)
                    if "scalar" in call:
                        waiting.append(lambda: nc.vector.scalar_tensor_tensor(out=made[:], **call))
                    else:
                        waiting.append(lambda: nc.vector.tensor_tensor(out=made[:], **call))
                    return made[:]

                y = bits[:].bitcast(F32)
                square = later("square", in0=y, in1=y, op=ALU.mult)
                a = later("a", in0=square, in1=w[:], op=ALU.mult)
                sum2 = later("sum2", in0=a, scalar=CUBIC[2], in1=a, op0=ALU.add, op1=ALU.mult)
                sum1 = later("sum1", in0=sum2, scalar=CUBIC[1], in1=a, op0=ALU.add, op1=ALU.mult)
                y = later("close", in0=sum1, scalar=CUBIC[0], in1=y, op0=ALU.add, op1=ALU.mult)
                square = later("square1", in0=y, scalar=-0.5 * LEAD**3 * UP, in1=y, op0=ALU.mult, op1=ALU.mult)
                a = later("a1", in0=square, in1=w[:], op=ALU.mult)
                y = later("rstd", in0=a, scalar=1.5 * LEAD * UP, in1=y, op0=ALU.add, op1=ALU.mult)
            shift = small.tile([P, columns], F32)

            def last_short():
                nc.vector.scalar_tensor_tensor(
                    out=shift[:], in0=mean, scalar=-1.0, in1=y, op0=ALU.mult, op1=ALU.mult
                )
                for j, i in enumerate(tiles):
                    affine_of[i] = (y, shift, j * HEADS)

            waiting.append(last_short)

        def normalise(i):
            while i not in affine_of:
                waiting.pop(0)()
            rstd, shift, first = affine_of[i]
            cat = work.tile([P, GROUPS, PACK, P], F32)
            for head in range(HEADS):
                g, j = divmod(head, HEADS_PER_GROUP)
                nc.scalar.activation(
                    out=cat[:, g, :, j * QUARTER : (j + 1) * QUARTER],
                    in_=ret_sb[i][:, head * HEAD : (head + 1) * HEAD].rearrange(
                        "p (c t) -> p t c", t=PACK
                    ),
                    func=ACT.Identity,
                    scale=rstd[:, first + head : first + head + 1],
                    bias=shift[:, first + head : first + head + 1],
                )
            cat_of[i] = cat

        def transpose_cat(i, g):
            ct = psum_c.tile([P, PACK, P], F32, tag="ct")
            for t in range(PACK):
                nc.tensor.transpose(
                    out=ct[:, t, :], in_=cat_of[i][:, g, t, :], identity=ident[:]
                )
            ct_of.setdefault(i, []).append(ct)

        def transpose_x(i):
            x_words = x_sb[i][:].bitcast(F32)
            pairs = K_PASS // 2
            if i in ():
                xt = psum_o.tile([P, GROUPS, 2, P], F32, tag="o")
            else:
                xt = psum_x.tile([P, GROUPS, 2, P], F32, tag="xt")
            for g in range(GROUPS):
                for u in range(2):
                    nc.tensor.transpose(
                        out=xt[:, g, u, :],
                        in_=x_words[:, g * pairs + u : (g + 1) * pairs : 2],
                        identity=ident[:],
                    )
            xt_of[i] = xt

        def group_x(i):
            x_grouped = work.tile([P, GROUPS * P * PACK], BF16, align_bytes=64)
            nc.scalar.copy(
                out=x_grouped[:].bitcast(F32).rearrange("p (g r u) -> p g r u", g=GROUPS, u=2),
                in_=xt_of[i][:].rearrange("p g u r -> p g r u"),
            )
            xg_of[i] = x_grouped

        def quantise_x(i):
            xq_words = work.tile([P, GROUPS, P], U32, align_bytes=64)
            xq_scales = work.tile([P, GROUPS, P], U8, align_bytes=64)
            nc.vector.quantize_mx(
                out=xq_words[:].rearrange("p g r -> p (g r)").bitcast(FP8X4),
                scales=xq_scales[:].rearrange("p g r -> p (g r)"),
                in_=xg_of[i][:],
            )
            xq_of[i] = (xq_words, xq_scales)
            one_short()

        def gate_half(i, n):
            xq_words, xq_scales = xq_of[i]
            zt = psum_z.tile([P, PACK, P], F32)
            for t in range(PACK):
                columns = slice(n * BANK + t * P, n * BANK + (t + 1) * P)
                for g in range(GROUPS):
                    nc.tensor.matmul_mx(
                        out=zt[:, t, :],
                        lhsT=wg_words[:, g, columns].bitcast(FP8X4),
                        lhsT_scale=wg_planes[PACK * g : P, columns],
                        rhs=xq_words[:, g, :].bitcast(FP8X4),
                        rhs_scale=xq_scales[:, g, :],
                        start=(g == 0),
                        stop=(g == GROUPS - 1),
                    )
            zt_of.setdefault(i, []).append(zt)

        def gate_matmul(i):
            for n in range(GROUPS):
                gate_half(i, n)

        def silu_half(i, n):
            gate = halves.tile([P, PACK, P], F32, bufs=4)
            for t in range(PACK):
                nc.scalar.activation(
                    out=gate[:, t, :], in_=zt_of[i][n][:, t, :], func=ACT.Silu,
                    bias=bg_columns[:, n, t : t + 1],
                )
            gate_of.setdefault(i, []).append(gate)

        def silu(i):
            for n in range(GROUPS):
                silu_half(i, n)

        def product_half(i, g):
            h = halves.tile([P, P, PACK], BF16, align_bytes=64)
            nc.vector.tensor_tensor(
                out=h[:].rearrange("p (c k) t -> p c t k", k=RUN),
                in0=ct_of[i][g][:].rearrange("p t (c k) -> p c t k", k=RUN),
                in1=gate_of[i][g][:].rearrange("p t (c k) -> p c t k", k=RUN),
                op=ALU.mult,
            )
            h_of.setdefault(i, []).append(h)
            one_short()

        def quantise_h(i, g):
            hq_words = halves.tile([P, P], U32, align_bytes=64)
            hq_scales = halves.tile([P, P], U8, align_bytes=64)
            nc.vector.quantize_mx(
                out=hq_words[:].bitcast(FP8X4),
                scales=hq_scales[:],
                in_=h_of[i][g][:].rearrange("p r t -> p (r t)"),
            )
            hq_of.setdefault(i, []).append((hq_words, hq_scales))
            one_short()

        def project(i):
            if i == TILES - 1:
                o_of[i] = [psum_c.tile([P, BANK], F32, name="o%d" % n, tag="ct") for n in range(GROUPS)]
            else:
                o_of[i] = [psum_o.tile([P, BANK], F32, name="o%d" % n, tag="o") for n in range(GROUPS)]
            for g in range(GROUPS):
                hq_words, hq_scales = hq_of[i][g]
                for n in range(GROUPS):
                    nc.tensor.matmul_mx(
                        out=o_of[i][n][:],
                        lhsT=hq_words[:].bitcast(FP8X4),
                        lhsT_scale=hq_scales[:],
                        rhs=wo_words[:, g, n * BANK : (n + 1) * BANK].bitcast(FP8X4),
                        rhs_scale=wo_planes[PACK * g : P, n * BANK : (n + 1) * BANK],
                        start=(g == 0),
                        stop=(g == GROUPS - 1),
                    )

        def add_bo_and_store(i, n):
            result = halves.tile([P, BANK], F32, bufs=8)
            nc.vector.tensor_tensor(
                out=result[:], in0=o_of[i][n][:], in1=bo_all[:, n], op=ALU.add
            )
            one_short()
            nc.sync.dma_start(out=out_rows[:, i, n * BANK : (n + 1) * BANK], in_=result[:])

        def scalar_add(i, n):
            copied = halves.tile([P, BANK], F32)
            nc.scalar.copy(out=copied[:], in_=o_of[i][n][:])
            summed = halves.tile([P, BANK], F32)
            nc.gpsimd.tensor_tensor(out=summed[:], in0=copied[:], in1=bo_all[:, n], op=ALU.add)
            nc.sync.dma_start(out=out_rows[:, i, n * BANK : (n + 1) * BANK], in_=summed[:])

        def each(step, i):
            if 0 <= i < TILES:
                step(i)

        statistics(0)
        transpose_x(0)
        group_x(0)
        statistics(1)
        sort_planes(0)
        sort_words(0)
        quantise_x(0)
        sort_planes(1)
        sort_words(1)
        gate_half(0, 0)
        transpose_x(1)
        gate_half(0, 1)
        warm_tensor()
        normalise(0)
        silu_half(0, 0)
        group_x(1)
        statistics(2)
        silu_half(0, 1)
        transpose_cat(0, 0)
        transpose_cat(0, 1)
        statistics(3)
        one_short()
        quantise_x(1)
        one_short()
        transpose_x(2)
        group_x(2)
        normalise(1)
        spread_bo()
        statistics(4)
        product_half(0, 0)
        product_half(0, 1)
        quantise_x(2)
        transpose_x(3)
        group_x(3)
        gate_half(1, 0)
        gate_half(1, 1)
        silu_half(1, 0)
        silu_half(1, 1)
        keep_bo()
        quantise_h(0, 0)
        quantise_h(0, 1)
        transpose_cat(1, 0)
        transpose_cat(1, 1)
        normalise(2)
        statistics(5)
        product_half(1, 0)
        product_half(1, 1)
        quantise_x(3)
        transpose_x(4)
        group_x(4)
        gate_half(2, 0)
        gate_half(2, 1)
        silu_half(2, 0)
        silu_half(2, 1)
        quantise_h(1, 0)
        quantise_h(1, 1)
        project(0)
        transpose_cat(2, 0)
        transpose_cat(2, 1)
        add_bo_and_store(0, 0)
        add_bo_and_store(0, 1)
        normalise(3)
        product_half(2, 0)
        product_half(2, 1)
        quantise_x(4)
        transpose_x(5)
        group_x(5)
        gate_half(3, 0)
        gate_half(3, 1)
        silu_half(3, 0)
        silu_half(3, 1)
        quantise_h(2, 0)
        quantise_h(2, 1)
        project(1)
        transpose_cat(3, 0)
        transpose_cat(3, 1)
        scalar_add(1, 0)
        scalar_add(1, 1)
        normalise(4)
        statistics(6)
        statistics(7)
        product_half(3, 0)
        product_half(3, 1)
        quantise_x(5)
        transpose_x(6)
        group_x(6)
        gate_half(4, 0)
        gate_half(4, 1)
        silu_half(4, 0)
        silu_half(4, 1)
        quantise_h(3, 0)
        quantise_h(3, 1)
        project(2)
        transpose_cat(4, 0)
        transpose_cat(4, 1)
        add_bo_and_store(2, 0)
        scalar_add(2, 1)
        normalise(5)
        product_half(4, 0)
        product_half(4, 1)
        quantise_x(6)
        transpose_x(7)
        group_x(7)
        gate_half(5, 0)
        gate_half(5, 1)
        silu_half(5, 0)
        silu_half(5, 1)
        quantise_h(4, 0)
        quantise_h(4, 1)
        project(3)
        transpose_cat(5, 0)
        transpose_cat(5, 1)
        add_bo_and_store(3, 0)
        scalar_add(3, 1)
        normalise(6)
        product_half(5, 0)
        product_half(5, 1)
        quantise_x(7)
        gate_half(6, 0)
        gate_half(6, 1)
        silu_half(6, 0)
        silu_half(6, 1)
        quantise_h(5, 0)
        quantise_h(5, 1)
        project(4)
        transpose_cat(6, 0)
        transpose_cat(6, 1)
        add_bo_and_store(4, 0)
        add_bo_and_store(4, 1)
        normalise(7)
        product_half(6, 0)
        product_half(6, 1)
        gate_half(7, 0)
        gate_half(7, 1)
        silu_half(7, 0)
        silu_half(7, 1)
        quantise_h(6, 0)
        quantise_h(6, 1)
        project(5)
        transpose_cat(7, 0)
        transpose_cat(7, 1)
        add_bo_and_store(5, 0)
        add_bo_and_store(5, 1)
        product_half(7, 0)
        product_half(7, 1)
        quantise_h(7, 0)
        quantise_h(7, 1)
        project(6)
        add_bo_and_store(6, 0)
        add_bo_and_store(6, 1)
        project(7)
        add_bo_and_store(7, 0)
        add_bo_and_store(7, 1)
